import numpy as np
import ml_dtypes


def mxq(x, axis, fmt="e4m3"):
    dtype, down = {"e4m3": (ml_dtypes.float8_e4m3fn, 7), "e5m2": (ml_dtypes.float8_e5m2, 14)}[fmt]
    v = np.moveaxis(np.asarray(x, np.float32).astype(ml_dtypes.bfloat16).astype(np.float64), axis, -1)
    blocks = v.reshape(v.shape[:-1] + (-1, 32))
    amax = np.abs(blocks).max(-1, keepdims=True)
    byte = np.maximum(np.where(amax > 0, np.frexp(amax)[1] - 1 + 127, 0) - down, 1)
    scale = np.exp2(byte - 127.0)
    codes = (blocks / scale).astype(np.float32).astype(dtype).astype(np.float64)
    return np.moveaxis((codes * scale).reshape(v.shape), -1, axis)


WIDE = False


def mx_kscale(k):
    if not WIDE:
        return np.ones(k)
    levels = np.array([10, -10, 5, -5, 0])
    a = np.random.permutation(np.resize(levels, k // 512 * 4)).reshape(k // 512, 4)
    idx = np.arange(k)
    return np.exp2(a[idx // 512, idx % 128 // 32])


BF16 = ml_dtypes.bfloat16


def bf(x):
    return np.asarray(x, np.float32).astype(BF16)


def f64(x):
    return np.asarray(x).astype(np.float64)


N, C_IN, H, W, C_OUT, K, POOL = 4, 512, 32, 32, 512, 3, 2
SUBTRACT_VALUE = 0.5
NEG_INIT = -1000000000.0
PAD = K // 2
HP, WP = H // POOL, W // POOL


def setup_inputs():
    s = mx_kscale(C_IN)[None, :, None, None]
    x = (np.random.standard_normal((N, C_IN, H, W)) + 0.5) * s
    weight = (np.random.standard_normal((C_OUT, C_IN, K, K)) * 1.8 / np.sqrt(C_IN) - 4.0 / C_IN) / s
    bias = 2.0 + 0.5 * np.random.standard_normal(C_OUT)
    return {"x": bf(x), "weight": bf(weight), "bias": bf(bias)}


def reference(x, weight, bias):
    xq = mxq(f64(x), 1, "e4m3")
    wq = mxq(f64(weight), 1, "e4m3")
    b = f64(bias)
    max_val = np.full((N, C_OUT, HP, WP), NEG_INIT)
    for kh in range(K):
        for kw in range(K):
            sh, rh = (kh - PAD) // POOL, (kh - PAD) % POOL
            sw, rw = (kw - PAD) // POOL, (kw - PAD) % POOL
            xs = xq[:, :, rh::POOL, rw::POOL]
            t = (wq[:, :, kh, kw] @ xs.reshape(N, C_IN, HP * WP)).reshape(N, C_OUT, HP, WP)
            t = t + b[None, :, None, None] - SUBTRACT_VALUE
            hs = t * np.clip(t + 3.0, 0.0, 6.0) / 6.0
            p0, p1 = max(0, -sh), min(HP, HP - sh)
            q0, q1 = max(0, -sw), min(WP, WP - sw)
            max_val[:, :, p0:p1, q0:q1] = np.maximum(max_val[:, :, p0:p1, q0:q1], hs[:, :, p0 + sh:p1 + sh, q0 + sw:q1 + sw])
    return max_val * np.tanh(np.log(1.0 + np.exp(max_val)))

@@ -1,0 +1,194 @@
+from contextlib import ExitStack
+
+import concourse.mybir as mybir
+
+F32 = mybir.dt.float32
+BF16 = mybir.dt.bfloat16
+U32 = mybir.dt.uint32
+U8 = mybir.dt.uint8
+FP8X4 = mybir.dt.float8_e4m3fn_x4
+ALU = mybir.AluOpType
+ACT = mybir.ActivationFunctionType
+
+P = 128
+PACK = 4
+IMAGES, C_IN, SIDE = 4, 512, 32
+C_OUT, KERNEL = 512, 3
+TAPS = KERNEL * KERNEL
+OUT_SIDE = SIDE // 2
+OUT_PIXELS = OUT_SIDE * OUT_SIDE
+PAIR = 2
+PAIRS = IMAGES // PAIR
+COLS = PAIR * OUT_PIXELS
+O_TILES = C_OUT // P
+W_CHUNK = 64
+W_RUN = PACK * TAPS
+W_SLOT = 48
+W_RAW_BUFS = 6
+EXP_CAP = 20.0
+
+FLOPS = 2 * TAPS * IMAGES * OUT_PIXELS * C_OUT * C_IN
+
+
+def tap_geometry(k):
+    shift, parity = divmod(k - 1, 2)
+    return shift, parity
+
+
+def tile_modelnew_pa_kernel(tc, x, weight, bias, out):
+    nc = tc.nc
+    with ExitStack() as stack:
+        keep = stack.enter_context(tc.tile_pool(name="keep", bufs=1))
+        x_stage = stack.enter_context(tc.tile_pool(name="x_stage", bufs=3))
+        w_stage = stack.enter_context(tc.tile_pool(name="w_stage", bufs=2))
+        w_ready = stack.enter_context(tc.tile_pool(name="w_ready", bufs=2))
+        stats = stack.enter_context(tc.tile_pool(name="stats", bufs=3))
+        results = stack.enter_context(tc.tile_pool(name="results", bufs=PAIRS * O_TILES))
+        psum = stack.enter_context(tc.psum_pool(name="psum", bufs=8))
+
+        x_raw = []
+        for n in range(IMAGES):
+            raw = keep.tile([P, PACK, SIDE * SIDE], BF16, name="x_raw%d" % n)
+            nc.sync.dma_start(out=raw, in_=x[n].rearrange("(p j) h w -> p j (h w)", j=PACK))
+            x_raw.append(raw)
+
+        bias_bf = keep.tile([P, O_TILES], BF16, name="bias_bf")
+        with nc.allow_non_contiguous_dma(reason="512 bias values, one to a partition and o-tile"):
+            nc.scalar.dma_start(out=bias_bf, in_=bias.rearrange("(k p) -> p k", p=P))
+
+        w_view = weight.rearrange("o (p j) kh kw -> p o (j kh kw)", j=PACK)
+        w_raw = []
+        for chunk in range(C_OUT // W_CHUNK):
+            raw = w_stage.tile([P, W_CHUNK, W_SLOT], BF16, name="w_raw", bufs=W_RAW_BUFS)
+            nc.sync.dma_start(
+                out=raw[:, :, 0:W_RUN], in_=w_view[:, chunk * W_CHUNK : (chunk + 1) * W_CHUNK, :]
+            )
+            w_raw.append(raw)
+
+        bias_t = keep.tile([P, O_TILES], F32, name="bias_t")
+        bias_t3 = keep.tile([P, O_TILES], F32, name="bias_t3")
+        nc.vector.tensor_scalar_add(out=bias_t, in0=bias_bf, scalar1=-0.5)
+        nc.vector.tensor_scalar_add(out=bias_t3, in0=bias_bf, scalar1=2.5)
+
+        x_codes = keep.tile([P, PAIRS, 4, COLS], U32, name="x_codes", align_bytes=64)
+        x_scales = keep.tile([P, PAIRS, 4, COLS], U8, name="x_scales", align_bytes=64)
+        for pair in range(PAIRS):
+            for row_parity in range(2):
+                for col_parity in range(2):
+                    grouped = x_stage.tile([P, PAIR, OUT_PIXELS, PACK], BF16, name="x_grouped", align_bytes=64)
+                    for i in range(PAIR):
+                        by_parity = x_raw[pair * PAIR + i].rearrange(
+                            "p j (a r b s) -> p r s a b j", r=2, b=OUT_SIDE, s=2
+                        )
+                        nc.vector.tensor_copy(
+                            out=grouped[:, i].rearrange("p (a b) j -> p a b j", b=OUT_SIDE),
+                            in_=by_parity[:, row_parity, col_parity],
+                        )
+                    which = 2 * row_parity + col_parity
+                    nc.vector.quantize_mx(
+                        out=x_codes[:, pair, which, :].bitcast(FP8X4),
+                        scales=x_scales[:, pair, which, :],
+                        in_=grouped.rearrange("p i x j -> p (i x j)"),
+                    )
+
+        def prepare_weights(o_tile):
+            grouped = w_stage.tile([P, TAPS, P, PACK], BF16, name="w_grouped", align_bytes=64)
+            chunks = P // W_CHUNK
+            for h in range(chunks):
+                raw = w_raw[o_tile * chunks + h]
+                nc.gpsimd.tensor_scalar(
+                    out=grouped[:, :, h * W_CHUNK : (h + 1) * W_CHUNK, :],
+                    in0=raw[:, :, 0:W_RUN].rearrange("p o (j t) -> p t o j", t=TAPS),
+                    scalar1=1.0,
+                    scalar2=0.0,
+                    op0=ALU.mult,
+                    op1=ALU.add,
+                )
+            codes = w_ready.tile([P, TAPS, P], U32, name="w_codes", align_bytes=64)
+            scales = w_ready.tile([P, TAPS, P], U8, name="w_scales", align_bytes=64)
+            for t in range(TAPS):
+                nc.vector.quantize_mx(
+                    out=codes[:, t, :].bitcast(FP8X4),
+                    scales=scales[:, t, :],
+                    in_=grouped[:, t].rearrange("p o j -> p (o j)"),
+                )
+            return codes, scales
+
+        def as_images(flat):
+            return flat.rearrange("p (i a b) -> p i a b", i=PAIR, a=OUT_SIDE)
+
+        def extremes_over_taps(w_codes, w_scales, pair):
+            first = stats.tile([P, COLS], F32, name="first")
+            largest = stats.tile([P, COLS], F32, name="largest")
+            smallest = stats.tile([P, COLS], F32, name="smallest")
+            count = 0
+            for kh in (1, 2, 0):
+                for kw in (1, 2, 0):
+                    row_shift, row_parity = tap_geometry(kh)
+                    col_shift, col_parity = tap_geometry(kw)
+                    which = 2 * row_parity + col_parity
+                    t = kh * KERNEL + kw
+                    sums = psum.tile([P, COLS], F32, name="sums")
+                    nc.tensor.matmul_mx(
+                        out=sums,
+                        lhsT=w_codes[:, t, :].bitcast(FP8X4),
+                        lhsT_scale=w_scales[:, t, :],
+                        rhs=x_codes[:, pair, which, :].bitcast(FP8X4),
+                        rhs_scale=x_scales[:, pair, which, :],
+                        start=True,
+                        stop=True,
+                    )
+                    if count == 0:
+                        nc.scalar.copy(out=first, in_=sums)
+                    elif count == 1:
+                        nc.vector.tensor_tensor(out=largest, in0=sums, in1=first, op=ALU.max)
+                        nc.vector.tensor_tensor(out=smallest, in0=sums, in1=first, op=ALU.min)
+                    else:
+                        src = as_images(sums)[
+                            :, :, 0 : OUT_SIDE + row_shift, 0 : OUT_SIDE + col_shift
+                        ]
+                        for running, op in ((largest, ALU.max), (smallest, ALU.min)):
+                            dst = as_images(running)[:, :, -row_shift:OUT_SIDE, -col_shift:OUT_SIDE]
+                            nc.vector.tensor_tensor(out=dst, in0=src, in1=dst, op=op)
+                    count += 1
+            return largest, smallest
+
+        def finish(o_tile, pair, largest, smallest):
+            b_t = bias_t[:, o_tile : o_tile + 1]
+            b_t3 = bias_t3[:, o_tile : o_tile + 1]
+            nc.scalar.activation(out=smallest, in_=smallest, func=ACT.Relu, bias=b_t3, scale=1.0)
+            nc.scalar.activation(out=largest, in_=largest, func=ACT.Identity, bias=b_t, scale=1.0)
+            best = largest
+            nc.vector.scalar_tensor_tensor(
+                out=best, in0=smallest, scalar=-1.0, in1=largest, op0=ALU.mult, op1=ALU.max
+            )
+            clipped = smallest
+            nc.vector.tensor_scalar(
+                out=clipped, in0=best, scalar1=3.0, scalar2=6.0, op0=ALU.add, op1=ALU.min
+            )
+            six_m = largest
+            nc.vector.tensor_tensor(out=six_m, in0=best, in1=clipped, op=ALU.mult)
+            gate = smallest
+            nc.scalar.activation(out=gate, in_=six_m, func=ACT.Relu, bias=EXP_CAP, scale=-1.0 / 6.0)
+            nc.scalar.activation(out=gate, in_=gate, func=ACT.Exp, bias=EXP_CAP, scale=-1.0)
+            nc.scalar.activation(out=gate, in_=gate, func=ACT.Ln, bias=1.0, scale=1.0)
+            nc.scalar.activation(out=gate, in_=gate, func=ACT.Tanh)
+            result = results.tile([P, COLS], F32, name="result")
+            nc.vector.scalar_tensor_tensor(
+                out=result, in0=six_m, scalar=1.0 / 6.0, in1=gate, op0=ALU.mult, op1=ALU.mult
+            )
+            nc.sync.dma_start(
+                out=out[pair * PAIR : (pair + 1) * PAIR, o_tile * P : (o_tile + 1) * P].rearrange(
+                    "i o a b -> o i (a b)"
+                ),
+                in_=result.rearrange("p (i x) -> p i x", i=PAIR),
+            )
+
+        ready = prepare_weights(0)
+        for o_tile in range(O_TILES):
+            w_codes, w_scales = ready
+            if o_tile + 1 < O_TILES:
+                ready = prepare_weights(o_tile + 1)
+            for pair in range(PAIRS):
+                largest, smallest = extremes_over_taps(w_codes, w_scales, pair)
+                finish(o_tile, pair, largest, smallest)

@@ -35,16 +35,29 @@ def tap_geometry(k):
     return shift, parity
 
 
+def as_images(flat):
+    return flat.rearrange("p (i a b) -> p i a b", i=PAIR, a=OUT_SIDE)
+
+
+def tap_source(sums, kh, kw):
+    return as_images(sums)[:, :, 0 : OUT_SIDE + tap_geometry(kh)[0], 0 : OUT_SIDE + tap_geometry(kw)[0]]
+
+
+def tap_target(running, kh, kw):
+    return as_images(running)[:, :, -tap_geometry(kh)[0] : OUT_SIDE, -tap_geometry(kw)[0] : OUT_SIDE]
+
+
 def tile_modelnew_pa_kernel(tc, x, weight, bias, out):
     nc = tc.nc
     with ExitStack() as stack:
         keep = stack.enter_context(tc.tile_pool(name="keep", bufs=1))
-        x_stage = stack.enter_context(tc.tile_pool(name="x_stage", bufs=3))
+        x_stage = stack.enter_context(tc.tile_pool(name="x_stage", bufs=8))
         w_stage = stack.enter_context(tc.tile_pool(name="w_stage", bufs=2))
         w_ready = stack.enter_context(tc.tile_pool(name="w_ready", bufs=2))
         stats = stack.enter_context(tc.tile_pool(name="stats", bufs=3))
-        results = stack.enter_context(tc.tile_pool(name="results", bufs=PAIRS * O_TILES))
+        batches = stack.enter_context(tc.tile_pool(name="batches", bufs=3))
         psum = stack.enter_context(tc.psum_pool(name="psum", bufs=8))
+        stack.enter_context(tc.manual_schedule())
 
         x_raw = []
         for n in range(IMAGES):
@@ -72,38 +85,49 @@ def tile_modelnew_pa_kernel(tc, x, weight, bias, out):
 
         x_codes = keep.tile([P, PAIRS, 4, COLS], U32, name="x_codes", align_bytes=64)
         x_scales = keep.tile([P, PAIRS, 4, COLS], U8, name="x_scales", align_bytes=64)
-        for pair in range(PAIRS):
-            for row_parity in range(2):
-                for col_parity in range(2):
-                    grouped = x_stage.tile([P, PAIR, OUT_PIXELS, PACK], BF16, name="x_grouped", align_bytes=64)
-                    for i in range(PAIR):
-                        by_parity = x_raw[pair * PAIR + i].rearrange(
-                            "p j (a r b s) -> p r s a b j", r=2, b=OUT_SIDE, s=2
-                        )
-                        nc.vector.tensor_copy(
-                            out=grouped[:, i].rearrange("p (a b) j -> p a b j", b=OUT_SIDE),
-                            in_=by_parity[:, row_parity, col_parity],
-                        )
-                    which = 2 * row_parity + col_parity
-                    nc.vector.quantize_mx(
-                        out=x_codes[:, pair, which, :].bitcast(FP8X4),
-                        scales=x_scales[:, pair, which, :],
-                        in_=grouped.rearrange("p i x j -> p (i x j)"),
-                    )
 
-        def prepare_weights(o_tile):
+        def regroup_x(copy, pair, which):
+            grouped = x_stage.tile([P, PAIR, OUT_PIXELS, PACK], BF16, name="x_grouped", align_bytes=64)
+            for i in range(PAIR):
+                by_parity = x_raw[pair * PAIR + i].rearrange(
+                    "p j (a r b s) -> p r s a b j", r=2, b=OUT_SIDE, s=2
+                )
+                copy(
+                    out=grouped[:, i].rearrange("p (a b) j -> p a b j", b=OUT_SIDE),
+                    in_=by_parity[:, which // 2, which % 2],
+                )
+            return grouped
+
+        def quantise_x(grouped, pair, which):
+            nc.vector.quantize_mx(
+                out=x_codes[:, pair, which, :].bitcast(FP8X4),
+                scales=x_scales[:, pair, which, :],
+                in_=grouped.rearrange("p i x j -> p (i x j)"),
+            )
+
+        first_pair = [regroup_x(nc.vector.tensor_copy, 0, 0)]
+        for which in range(1, 4):
+            first_pair.append(regroup_x(nc.vector.tensor_copy, 0, which))
+            quantise_x(first_pair[which - 1], 0, which - 1)
+        quantise_x(first_pair[3], 0, 3)
+        for which in range(4):
+            quantise_x(regroup_x(nc.scalar.copy, 1, which), 1, which)
+
+        def regroup_weights(o_tile):
             grouped = w_stage.tile([P, TAPS, P, PACK], BF16, name="w_grouped", align_bytes=64)
             chunks = P // W_CHUNK
             for h in range(chunks):
-                raw = w_raw[o_tile * chunks + h]
                 nc.gpsimd.tensor_scalar(
                     out=grouped[:, :, h * W_CHUNK : (h + 1) * W_CHUNK, :],
-                    in0=raw[:, :, 0:W_RUN].rearrange("p o (j t) -> p t o j", t=TAPS),
+                    in0=w_raw[o_tile * chunks + h][:, :, 0:W_RUN].rearrange("p o (j t) -> p t o j", t=TAPS),
                     scalar1=1.0,
                     scalar2=0.0,
                     op0=ALU.mult,
                     op1=ALU.add,
                 )
+            return grouped
+
+        def quantise_weights(grouped):
             codes = w_ready.tile([P, TAPS, P], U32, name="w_codes", align_bytes=64)
             scales = w_ready.tile([P, TAPS, P], U8, name="w_scales", align_bytes=64)
             for t in range(TAPS):
@@ -114,81 +138,180 @@ def tile_modelnew_pa_kernel(tc, x, weight, bias, out):
                 )
             return codes, scales
 
-        def as_images(flat):
-            return flat.rearrange("p (i a b) -> p i a b", i=PAIR, a=OUT_SIDE)
-
-        def extremes_over_taps(w_codes, w_scales, pair):
-            first = stats.tile([P, COLS], F32, name="first")
-            largest = stats.tile([P, COLS], F32, name="largest")
-            smallest = stats.tile([P, COLS], F32, name="smallest")
-            count = 0
-            for kh in (1, 2, 0):
-                for kw in (1, 2, 0):
-                    row_shift, row_parity = tap_geometry(kh)
-                    col_shift, col_parity = tap_geometry(kw)
-                    which = 2 * row_parity + col_parity
-                    t = kh * KERNEL + kw
-                    sums = psum.tile([P, COLS], F32, name="sums")
-                    nc.tensor.matmul_mx(
-                        out=sums,
-                        lhsT=w_codes[:, t, :].bitcast(FP8X4),
-                        lhsT_scale=w_scales[:, t, :],
-                        rhs=x_codes[:, pair, which, :].bitcast(FP8X4),
-                        rhs_scale=x_scales[:, pair, which, :],
-                        start=True,
-                        stop=True,
-                    )
-                    if count == 0:
-                        nc.scalar.copy(out=first, in_=sums)
-                    elif count == 1:
-                        nc.vector.tensor_tensor(out=largest, in0=sums, in1=first, op=ALU.max)
-                        nc.vector.tensor_tensor(out=smallest, in0=sums, in1=first, op=ALU.min)
-                    else:
-                        src = as_images(sums)[
-                            :, :, 0 : OUT_SIDE + row_shift, 0 : OUT_SIDE + col_shift
-                        ]
-                        for running, op in ((largest, ALU.max), (smallest, ALU.min)):
-                            dst = as_images(running)[:, :, -row_shift:OUT_SIDE, -col_shift:OUT_SIDE]
-                            nc.vector.tensor_tensor(out=dst, in0=src, in1=dst, op=op)
-                    count += 1
-            return largest, smallest
-
-        def finish(o_tile, pair, largest, smallest):
-            b_t = bias_t[:, o_tile : o_tile + 1]
-            b_t3 = bias_t3[:, o_tile : o_tile + 1]
-            nc.scalar.activation(out=smallest, in_=smallest, func=ACT.Relu, bias=b_t3, scale=1.0)
-            nc.scalar.activation(out=largest, in_=largest, func=ACT.Identity, bias=b_t, scale=1.0)
-            best = largest
-            nc.vector.scalar_tensor_tensor(
-                out=best, in0=smallest, scalar=-1.0, in1=largest, op0=ALU.mult, op1=ALU.max
+        def tap_sums(unit, kh, kw):
+            which = 2 * tap_geometry(kh)[1] + tap_geometry(kw)[1]
+            t = kh * KERNEL + kw
+            sums = psum.tile([P, COLS], F32, name="sums")
+            nc.tensor.matmul_mx(
+                out=sums,
+                lhsT=unit["codes"][:, t, :].bitcast(FP8X4),
+                lhsT_scale=unit["scales"][:, t, :],
+                rhs=x_codes[:, unit["pair"], which, :].bitcast(FP8X4),
+                rhs_scale=x_scales[:, unit["pair"], which, :],
+                start=True,
+                stop=True,
             )
-            clipped = smallest
-            nc.vector.tensor_scalar(
-                out=clipped, in0=best, scalar1=3.0, scalar2=6.0, op0=ALU.add, op1=ALU.min
+            return sums
+
+        def centre_tap(unit):
+            if unit is None:
+                return
+            nc.scalar.activation(
+                out=unit["largest"], in_=tap_sums(unit, 1, 1), func=ACT.Identity, bias=unit["bias_t"], scale=1.0
             )
-            six_m = largest
-            nc.vector.tensor_tensor(out=six_m, in0=best, in1=clipped, op=ALU.mult)
-            gate = smallest
-            nc.scalar.activation(out=gate, in_=six_m, func=ACT.Relu, bias=EXP_CAP, scale=-1.0 / 6.0)
-            nc.scalar.activation(out=gate, in_=gate, func=ACT.Exp, bias=EXP_CAP, scale=-1.0)
-            nc.scalar.activation(out=gate, in_=gate, func=ACT.Ln, bias=1.0, scale=1.0)
-            nc.scalar.activation(out=gate, in_=gate, func=ACT.Tanh)
-            result = results.tile([P, COLS], F32, name="result")
+
+        def cross_tap(unit, kh, kw, seed=False):
+            if unit is None:
+                return
+            source = tap_source(tap_sums(unit, kh, kw), kh, kw)
+            low = unit["largest"] if seed else unit["smallest"]
             nc.vector.scalar_tensor_tensor(
-                out=result, in0=six_m, scalar=1.0 / 6.0, in1=gate, op0=ALU.mult, op1=ALU.mult
+                out=tap_target(unit["smallest"], kh, kw), in0=source, scalar=unit["bias_t"],
+                in1=tap_target(low, kh, kw), op0=ALU.add, op1=ALU.min,
+            )
+            nc.vector.scalar_tensor_tensor(
+                out=tap_target(unit["largest"], kh, kw), in0=source, scalar=unit["bias_t"],
+                in1=tap_target(unit["largest"], kh, kw), op0=ALU.add, op1=ALU.max,
+            )
+
+        def fold_corner(unit, kh, kw, seed=False):
+            if unit is None:
+                return None
+            folded = unit["corner"] if seed else stats.tile([P, COLS], F32, name="folded", bufs=5)
+            nc.scalar.activation(
+                out=folded, in_=tap_sums(unit, kh, kw), func=ACT.Relu, bias=unit["bias_t3"], scale=1.0
+            )
+            nc.scalar.activation(out=folded, in_=folded, func=ACT.Abs, bias=-1.5, scale=1.0)
+            return folded
+
+        def corner_max(unit, folded, kh, kw):
+            if unit is None:
+                return
+            target = tap_target(unit["corner"], kh, kw)
+            nc.vector.tensor_tensor(out=target, in0=tap_source(folded, kh, kw), in1=target, op=ALU.max)
+
+        def relu_smallest(unit):
+            if unit is not None:
+                nc.scalar.activation(out=unit["smallest"], in_=unit["smallest"], func=ACT.Relu, bias=3.0, scale=1.0)
+
+        def best_of_extremes(unit):
+            if unit is not None:
+                nc.vector.scalar_tensor_tensor(
+                    out=unit["largest"], in0=unit["smallest"], scalar=-1.0, in1=unit["largest"],
+                    op0=ALU.mult, op1=ALU.max,
+                )
+
+        def merge_corners(unit):
+            if unit is not None:
+                nc.vector.scalar_tensor_tensor(
+                    out=unit["largest"], in0=unit["corner"], scalar=-1.5, in1=unit["largest"],
+                    op0=ALU.add, op1=ALU.max,
+                )
+
+        def clip(unit):
+            if unit is not None:
+                nc.vector.tensor_scalar(
+                    out=unit["smallest"], in0=unit["largest"], scalar1=3.0, scalar2=6.0, op0=ALU.add, op1=ALU.min
+                )
+
+        def hardswish_times_six(unit):
+            if unit is not None:
+                nc.vector.tensor_tensor(out=unit["six_m"], in0=unit["largest"], in1=unit["smallest"], op=ALU.mult)
+
+        def cap(unit):
+            if unit is not None:
+                nc.vector.tensor_scalar(
+                    out=unit["gate"], in0=unit["six_m"], scalar1=1.0 / 6.0, scalar2=EXP_CAP, op0=ALU.mult, op1=ALU.min
+                )
+
+        def exp_gate(unit):
+            if unit is not None:
+                nc.scalar.activation(out=unit["gate"], in_=unit["gate"], func=ACT.Exp)
+
+        def finish(o_tile, batch):
+            nc.vector.scalar_tensor_tensor(
+                out=batch["gate"], in0=batch["six_m"], scalar=1.0 / 6.0, in1=batch["gate"],
+                op0=ALU.mult, op1=ALU.mult,
             )
             nc.sync.dma_start(
-                out=out[pair * PAIR : (pair + 1) * PAIR, o_tile * P : (o_tile + 1) * P].rearrange(
-                    "i o a b -> o i (a b)"
-                ),
-                in_=result.rearrange("p (i x) -> p i x", i=PAIR),
+                out=out[:, o_tile * P : (o_tile + 1) * P].rearrange("n o a b -> o n (a b)"),
+                in_=batch["gate"].rearrange("p (n x) -> p n x", n=IMAGES),
             )
 
-        ready = prepare_weights(0)
-        for o_tile in range(O_TILES):
-            w_codes, w_scales = ready
-            if o_tile + 1 < O_TILES:
-                ready = prepare_weights(o_tile + 1)
-            for pair in range(PAIRS):
-                largest, smallest = extremes_over_taps(w_codes, w_scales, pair)
-                finish(o_tile, pair, largest, smallest)
+        n_units = O_TILES * PAIRS
+
+        def completed_o_tile(index):
+            if 0 <= index < n_units and index % PAIRS == PAIRS - 1:
+                return index // PAIRS
+            return None
+
+        def unit_or_none(index):
+            return units[index] if 0 <= index < len(units) else None
+
+        units = []
+        batch_tiles = []
+        ready = quantise_weights(regroup_weights(0))
+        grouped_next = None
+        for i in range(n_units + 3):
+            o_tile, pair = divmod(i, PAIRS)
+            if i < n_units:
+                if pair == 0:
+                    codes, scales = ready
+                    batch_tiles.append(
+                        {
+                            "six_m": batches.tile([P, PAIRS * COLS], F32, name="six_m"),
+                            "gate": batches.tile([P, PAIRS * COLS], F32, name="gate"),
+                        }
+                    )
+                    if o_tile + 1 < O_TILES:
+                        grouped_next = regroup_weights(o_tile + 1)
+                units.append(
+                    {
+                        "pair": pair,
+                        "codes": codes,
+                        "scales": scales,
+                        "bias_t": bias_t[:, o_tile : o_tile + 1],
+                        "bias_t3": bias_t3[:, o_tile : o_tile + 1],
+                        "largest": stats.tile([P, COLS], F32, name="largest"),
+                        "smallest": stats.tile([P, COLS], F32, name="smallest"),
+                        "corner": stats.tile([P, COLS], F32, name="corner"),
+                        "six_m": batch_tiles[o_tile]["six_m"][:, pair * COLS : (pair + 1) * COLS],
+                        "gate": batch_tiles[o_tile]["gate"][:, pair * COLS : (pair + 1) * COLS],
+                    }
+                )
+            now = unit_or_none(i)
+            before = unit_or_none(i - 1)
+
+            centre_tap(now)
+            cross_tap(now, 1, 2, seed=True)
+            fold_corner(now, 2, 2, seed=True)
+            cross_tap(now, 2, 1)
+            folded_20 = fold_corner(now, 2, 0)
+
+            relu_smallest(before)
+            closing = completed_o_tile(i - 3)
+            if closing is not None:
+                gate = batch_tiles[closing]["gate"]
+                nc.scalar.activation(out=gate, in_=gate, func=ACT.Tanh)
+            exp_gate(unit_or_none(i - 2))
+
+            best_of_extremes(before)
+            cross_tap(now, 1, 0)
+            merge_corners(before)
+            if now is not None and pair == PAIRS - 1 and o_tile + 1 < O_TILES:
+                ready = quantise_weights(grouped_next)
+            folded_02 = fold_corner(now, 0, 2)
+            cross_tap(now, 0, 1)
+            clip(before)
+            folded_00 = fold_corner(now, 0, 0)
+            corner_max(now, folded_20, 2, 0)
+            hardswish_times_six(before)
+            corner_max(now, folded_02, 0, 2)
+            cap(before)
+            corner_max(now, folded_00, 0, 0)
+
+            if completed_o_tile(i - 2) is not None:
+                gate = batch_tiles[completed_o_tile(i - 2)]["gate"]
+                nc.scalar.activation(out=gate, in_=gate, func=ACT.Ln, bias=1.0, scale=1.0)
+            if closing is not None:
+                finish(closing, batch_tiles[closing])

@@ -1,6 +1,7 @@
 from contextlib import ExitStack
 
 import concourse.mybir as mybir
+from concourse.masks import make_identity
 
 F32 = mybir.dt.float32
 BF16 = mybir.dt.bfloat16
@@ -21,10 +22,9 @@ PAIR = 2
 PAIRS = IMAGES // PAIR
 COLS = PAIR * OUT_PIXELS
 O_TILES = C_OUT // P
-W_CHUNK = 64
-W_RUN = PACK * TAPS
-W_SLOT = 48
-W_RAW_BUFS = 6
+HALVES = 2
+BUNCH = 2
+BUNCHES = (TAPS + BUNCH - 1) // BUNCH
 EXP_CAP = 20.0
 
 FLOPS = 2 * TAPS * IMAGES * OUT_PIXELS * C_OUT * C_IN
@@ -51,52 +51,97 @@ def tile_modelnew_pa_kernel(tc, x, weight, bias, out):
     nc = tc.nc
     with ExitStack() as stack:
         keep = stack.enter_context(tc.tile_pool(name="keep", bufs=1))
-        x_stage = stack.enter_context(tc.tile_pool(name="x_stage", bufs=8))
+        x_stage = stack.enter_context(tc.tile_pool(name="x_stage", bufs=5))
         w_stage = stack.enter_context(tc.tile_pool(name="w_stage", bufs=2))
         w_ready = stack.enter_context(tc.tile_pool(name="w_ready", bufs=2))
         stats = stack.enter_context(tc.tile_pool(name="stats", bufs=3))
         batches = stack.enter_context(tc.tile_pool(name="batches", bufs=3))
-        psum = stack.enter_context(tc.psum_pool(name="psum", bufs=8))
+        psum = stack.enter_context(tc.psum_pool(name="psum", bufs=6))
+        psum_w = stack.enter_context(tc.psum_pool(name="psum_w", bufs=2))
         stack.enter_context(tc.manual_schedule())
 
-        x_raw = []
+        identity = keep.tile([P, P], F32, name="identity")
+        make_identity(nc, identity)
+
+        w_rows = [keep.tile([P, C_IN * TAPS], BF16, name="w_rows%d" % o_tile) for o_tile in range(O_TILES)]
+        x_raw = [keep.tile([P, PACK, SIDE * SIDE], BF16, name="x_raw%d" % n) for n in range(IMAGES)]
+
+        def load_weights(o_tile):
+            nc.sync.dma_start(
+                out=w_rows[o_tile],
+                in_=weight[o_tile * P : (o_tile + 1) * P].rearrange("o c kh kw -> o (c kh kw)"),
+            )
+
+        load_weights(0)
         for n in range(IMAGES):
-            raw = keep.tile([P, PACK, SIDE * SIDE], BF16, name="x_raw%d" % n)
-            nc.sync.dma_start(out=raw, in_=x[n].rearrange("(p j) h w -> p j (h w)", j=PACK))
-            x_raw.append(raw)
+            nc.sync.dma_start(
+                out=x_raw[n].rearrange("q (u e) s -> q u (e s)", u=HALVES),
+                in_=x[n].rearrange("(u q e) h w -> q u (e h w)", u=HALVES, q=P),
+            )
+        for o_tile in range(1, O_TILES):
+            load_weights(o_tile)
 
         bias_bf = keep.tile([P, O_TILES], BF16, name="bias_bf")
         with nc.allow_non_contiguous_dma(reason="512 bias values, one to a partition and o-tile"):
             nc.scalar.dma_start(out=bias_bf, in_=bias.rearrange("(k p) -> p k", p=P))
-
-        w_view = weight.rearrange("o (p j) kh kw -> p o (j kh kw)", j=PACK)
-        w_raw = []
-        for chunk in range(C_OUT // W_CHUNK):
-            raw = w_stage.tile([P, W_CHUNK, W_SLOT], BF16, name="w_raw", bufs=W_RAW_BUFS)
-            nc.sync.dma_start(
-                out=raw[:, :, 0:W_RUN], in_=w_view[:, chunk * W_CHUNK : (chunk + 1) * W_CHUNK, :]
-            )
-            w_raw.append(raw)
 
         bias_t = keep.tile([P, O_TILES], F32, name="bias_t")
         bias_t3 = keep.tile([P, O_TILES], F32, name="bias_t3")
         nc.vector.tensor_scalar_add(out=bias_t, in0=bias_bf, scalar1=-0.5)
         nc.vector.tensor_scalar_add(out=bias_t3, in0=bias_bf, scalar1=2.5)
 
+        def gpsimd_copy(out, in_):
+            nc.gpsimd.tensor_scalar(out=out, in0=in_, scalar1=1.0, scalar2=0.0, op0=ALU.mult, op1=ALU.add)
+
+        def sort_weights(o_tile):
+            by_tap = w_stage.tile([P, TAPS, C_IN], BF16, name="w_by_tap")
+            for t0 in range(0, TAPS, BUNCH):
+                t1 = min(t0 + BUNCH, TAPS)
+                gpsimd_copy(
+                    out=by_tap[:, t0:t1, :],
+                    in_=w_rows[o_tile].rearrange("o (c t) -> o t c", t=TAPS)[:, t0:t1, :],
+                )
+            return {
+                "by_tap": by_tap.rearrange("o t c -> o (t c)").bitcast(F32),
+                "grouped": w_stage.tile([P, TAPS, P * PACK], BF16, name="w_grouped", align_bytes=64),
+                "codes": w_ready.tile([P, TAPS, P], U32, name="w_codes", align_bytes=64),
+                "scales": w_ready.tile([P, TAPS, P], U8, name="w_scales", align_bytes=64),
+            }
+
+        def flip_weights(w, bunch):
+            if w is None or bunch >= BUNCHES:
+                return
+            t0, t1 = bunch * BUNCH, min((bunch + 1) * BUNCH, TAPS)
+            flipped = psum_w.tile([P, BUNCH, HALVES, P], F32, name="flipped")
+            for t in range(t0, t1):
+                for u in range(HALVES):
+                    first_word = (t * HALVES + u) * P
+                    nc.tensor.transpose(flipped[:, t - t0, u, :], w["by_tap"][:, first_word : first_word + P], identity)
+            words = w["grouped"][:, t0:t1, :].rearrange("q t k -> q (t k)").bitcast(F32)
+            nc.scalar.copy(
+                out=words.rearrange("q (t o u) -> q t o u", t=t1 - t0, u=HALVES),
+                in_=flipped[:, 0 : t1 - t0].rearrange("q t u o -> q t o u"),
+            )
+
+        def quantise_weights(w, bunch):
+            if w is None or bunch < 0 or bunch >= BUNCHES:
+                return
+            t0, t1 = bunch * BUNCH, min((bunch + 1) * BUNCH, TAPS)
+            nc.vector.quantize_mx(
+                out=w["codes"][:, t0:t1, :].rearrange("q t o -> q (t o)").bitcast(FP8X4),
+                scales=w["scales"][:, t0:t1, :].rearrange("q t o -> q (t o)"),
+                in_=w["grouped"][:, t0:t1, :].rearrange("q t k -> q (t k)"),
+            )
+
         x_codes = keep.tile([P, PAIRS, 4, COLS], U32, name="x_codes", align_bytes=64)
         x_scales = keep.tile([P, PAIRS, 4, COLS], U8, name="x_scales", align_bytes=64)
 
-        def regroup_x(copy, pair, which):
-            grouped = x_stage.tile([P, PAIR, OUT_PIXELS, PACK], BF16, name="x_grouped", align_bytes=64)
-            for i in range(PAIR):
-                by_parity = x_raw[pair * PAIR + i].rearrange(
-                    "p j (a r b s) -> p r s a b j", r=2, b=OUT_SIDE, s=2
-                )
-                copy(
-                    out=grouped[:, i].rearrange("p (a b) j -> p a b j", b=OUT_SIDE),
-                    in_=by_parity[:, which // 2, which % 2],
-                )
-            return grouped
+        def regroup_x(copy, grouped, n, which):
+            by_parity = x_raw[n].rearrange("p j (a r b s) -> p r s a b j", r=2, b=OUT_SIDE, s=2)
+            copy(
+                out=grouped[:, n % PAIR].rearrange("p (a b) j -> p a b j", b=OUT_SIDE),
+                in_=by_parity[:, which // 2, which % 2],
+            )
 
         def quantise_x(grouped, pair, which):
             nc.vector.quantize_mx(
@@ -105,38 +150,26 @@ def tile_modelnew_pa_kernel(tc, x, weight, bias, out):
                 in_=grouped.rearrange("p i x j -> p (i x j)"),
             )
 
-        first_pair = [regroup_x(nc.vector.tensor_copy, 0, 0)]
-        for which in range(1, 4):
-            first_pair.append(regroup_x(nc.vector.tensor_copy, 0, which))
-            quantise_x(first_pair[which - 1], 0, which - 1)
-        quantise_x(first_pair[3], 0, 3)
+        def new_x_tiles():
+            return [
+                x_stage.tile([P, PAIR, OUT_PIXELS, PACK], BF16, name="x_grouped%d" % which, bufs=2, align_bytes=64)
+                for which in range(4)
+            ]
+
+        weights_now = sort_weights(0)
+        x_first, x_second = new_x_tiles(), new_x_tiles()
+        for n in range(IMAGES):
+            for which in range(4):
+                if n < PAIR:
+                    regroup_x(nc.vector.tensor_copy, x_first[which], n, which)
+                else:
+                    regroup_x(gpsimd_copy, x_second[which], n, which)
+        for bunch in range(BUNCHES):
+            flip_weights(weights_now, bunch)
         for which in range(4):
-            quantise_x(regroup_x(nc.scalar.copy, 1, which), 1, which)
-
-        def regroup_weights(o_tile):
-            grouped = w_stage.tile([P, TAPS, P, PACK], BF16, name="w_grouped", align_bytes=64)
-            chunks = P // W_CHUNK
-            for h in range(chunks):
-                nc.gpsimd.tensor_scalar(
-                    out=grouped[:, :, h * W_CHUNK : (h + 1) * W_CHUNK, :],
-                    in0=w_raw[o_tile * chunks + h][:, :, 0:W_RUN].rearrange("p o (j t) -> p t o j", t=TAPS),
-                    scalar1=1.0,
-                    scalar2=0.0,
-                    op0=ALU.mult,
-                    op1=ALU.add,
-                )
-            return grouped
-
-        def quantise_weights(grouped):
-            codes = w_ready.tile([P, TAPS, P], U32, name="w_codes", align_bytes=64)
-            scales = w_ready.tile([P, TAPS, P], U8, name="w_scales", align_bytes=64)
-            for t in range(TAPS):
-                nc.vector.quantize_mx(
-                    out=codes[:, t, :].bitcast(FP8X4),
-                    scales=scales[:, t, :],
-                    in_=grouped[:, t].rearrange("p o j -> p (o j)"),
-                )
-            return codes, scales
+            quantise_x(x_first[which], 0, which)
+        for bunch in range(BUNCHES):
+            quantise_weights(weights_now, bunch)
 
         def tap_sums(unit, kh, kw):
             which = 2 * tap_geometry(kh)[1] + tap_geometry(kw)[1]
@@ -239,6 +272,7 @@ def tile_modelnew_pa_kernel(tc, x, weight, bias, out):
             )
 
         n_units = O_TILES * PAIRS
+        SITES = 3
 
         def completed_o_tile(index):
             if 0 <= index < n_units and index % PAIRS == PAIRS - 1:
@@ -250,26 +284,25 @@ def tile_modelnew_pa_kernel(tc, x, weight, bias, out):
 
         units = []
         batch_tiles = []
-        ready = quantise_weights(regroup_weights(0))
-        grouped_next = None
+        weights_next = None
         for i in range(n_units + 3):
             o_tile, pair = divmod(i, PAIRS)
             if i < n_units:
                 if pair == 0:
-                    codes, scales = ready
+                    if o_tile > 0:
+                        weights_now = weights_next
+                    weights_next = sort_weights(o_tile + 1) if o_tile + 1 < O_TILES else None
                     batch_tiles.append(
                         {
                             "six_m": batches.tile([P, PAIRS * COLS], F32, name="six_m"),
                             "gate": batches.tile([P, PAIRS * COLS], F32, name="gate"),
                         }
                     )
-                    if o_tile + 1 < O_TILES:
-                        grouped_next = regroup_weights(o_tile + 1)
                 units.append(
                     {
                         "pair": pair,
-                        "codes": codes,
-                        "scales": scales,
+                        "codes": weights_now["codes"],
+                        "scales": weights_now["scales"],
                         "bias_t": bias_t[:, o_tile : o_tile + 1],
                         "bias_t3": bias_t3[:, o_tile : o_tile + 1],
                         "largest": stats.tile([P, COLS], F32, name="largest"),
@@ -279,13 +312,18 @@ def tile_modelnew_pa_kernel(tc, x, weight, bias, out):
                         "gate": batch_tiles[o_tile]["gate"][:, pair * COLS : (pair + 1) * COLS],
                     }
                 )
+            else:
+                weights_next = None
             now = unit_or_none(i)
             before = unit_or_none(i - 1)
+            bunch = pair * SITES
 
             centre_tap(now)
             cross_tap(now, 1, 2, seed=True)
             fold_corner(now, 2, 2, seed=True)
             cross_tap(now, 2, 1)
+            quantise_weights(weights_next, bunch - 1)
+            flip_weights(weights_next, bunch)
             folded_20 = fold_corner(now, 2, 0)
 
             relu_smallest(before)
@@ -298,11 +336,13 @@ def tile_modelnew_pa_kernel(tc, x, weight, bias, out):
             best_of_extremes(before)
             cross_tap(now, 1, 0)
             merge_corners(before)
-            if now is not None and pair == PAIRS - 1 and o_tile + 1 < O_TILES:
-                ready = quantise_weights(grouped_next)
+            quantise_weights(weights_next, bunch)
+            flip_weights(weights_next, bunch + 1)
             folded_02 = fold_corner(now, 0, 2)
             cross_tap(now, 0, 1)
             clip(before)
+            quantise_weights(weights_next, bunch + 1)
+            flip_weights(weights_next, bunch + 2)
             folded_00 = fold_corner(now, 0, 0)
             corner_max(now, folded_20, 2, 0)
             hardswish_times_six(before)
@@ -310,6 +350,9 @@ def tile_modelnew_pa_kernel(tc, x, weight, bias, out):
             cap(before)
             corner_max(now, folded_00, 0, 0)
 
+            if i == 0:
+                for which in range(4):
+                    quantise_x(x_second[which], 1, which)
             if completed_o_tile(i - 2) is not None:
                 gate = batch_tiles[completed_o_tile(i - 2)]["gate"]
                 nc.scalar.activation(out=gate, in_=gate, func=ACT.Ln, bias=1.0, scale=1.0)

@@ -25,6 +25,8 @@ O_TILES = C_OUT // P
 HALVES = 2
 BUNCH = 2
 BUNCHES = (TAPS + BUNCH - 1) // BUNCH
+SORT_GROUP = 4
+SORT_GROUPS = (TAPS + SORT_GROUP - 1) // SORT_GROUP
 EXP_CAP = 20.0
 
 FLOPS = 2 * TAPS * IMAGES * OUT_PIXELS * C_OUT * C_IN
@@ -90,33 +92,34 @@ def tile_modelnew_pa_kernel(tc, x, weight, bias, out):
         nc.vector.tensor_scalar_add(out=bias_t, in0=bias_bf, scalar1=-0.5)
         nc.vector.tensor_scalar_add(out=bias_t3, in0=bias_bf, scalar1=2.5)
 
-        def gpsimd_copy(out, in_):
-            nc.gpsimd.tensor_scalar(out=out, in0=in_, scalar1=1.0, scalar2=0.0, op0=ALU.mult, op1=ALU.add)
-
-        def sort_weights(o_tile):
+        def new_weights(o_tile):
             by_tap = w_stage.tile([P, TAPS, C_IN], BF16, name="w_by_tap")
-            for t0 in range(0, TAPS, BUNCH):
-                t1 = min(t0 + BUNCH, TAPS)
-                gpsimd_copy(
-                    out=by_tap[:, t0:t1, :],
-                    in_=w_rows[o_tile].rearrange("o (c t) -> o t c", t=TAPS)[:, t0:t1, :],
-                )
             return {
-                "by_tap": by_tap.rearrange("o t c -> o (t c)").bitcast(F32),
+                "rows": w_rows[o_tile].rearrange("o (c t) -> o c t", t=TAPS),
+                "by_tap": by_tap,
+                "by_tap_words": by_tap.rearrange("o t c -> o (t c)").bitcast(F32),
                 "grouped": w_stage.tile([P, TAPS, P * PACK], BF16, name="w_grouped", align_bytes=64),
                 "codes": w_ready.tile([P, TAPS, P], U32, name="w_codes", align_bytes=64),
                 "scales": w_ready.tile([P, TAPS, P], U8, name="w_scales", align_bytes=64),
             }
 
+        def sort_weights(w, group):
+            if w is None or group < 0 or group >= SORT_GROUPS:
+                return
+            t0, t1 = group * SORT_GROUP, min((group + 1) * SORT_GROUP, TAPS)
+            nc.vector.tensor_copy(
+                out=w["by_tap"][:, t0:t1, :].rearrange("o t c -> o c t"), in_=w["rows"][:, :, t0:t1]
+            )
+
         def flip_weights(w, bunch):
-            if w is None or bunch >= BUNCHES:
+            if w is None or bunch < 0 or bunch >= BUNCHES:
                 return
             t0, t1 = bunch * BUNCH, min((bunch + 1) * BUNCH, TAPS)
             flipped = psum_w.tile([P, BUNCH, HALVES, P], F32, name="flipped")
             for t in range(t0, t1):
                 for u in range(HALVES):
                     first_word = (t * HALVES + u) * P
-                    nc.tensor.transpose(flipped[:, t - t0, u, :], w["by_tap"][:, first_word : first_word + P], identity)
+                    nc.tensor.transpose(flipped[:, t - t0, u, :], w["by_tap_words"][:, first_word : first_word + P], identity)
             words = w["grouped"][:, t0:t1, :].rearrange("q t k -> q (t k)").bitcast(F32)
             nc.scalar.copy(
                 out=words.rearrange("q (t o u) -> q t o u", t=t1 - t0, u=HALVES),
@@ -156,16 +159,18 @@ def tile_modelnew_pa_kernel(tc, x, weight, bias, out):
                 for which in range(4)
             ]
 
-        weights_now = sort_weights(0)
+        weights_now = new_weights(0)
+        for group in range(SORT_GROUPS):
+            sort_weights(weights_now, group)
+        for bunch in range(BUNCHES):
+            flip_weights(weights_now, bunch)
         x_first, x_second = new_x_tiles(), new_x_tiles()
         for n in range(IMAGES):
             for which in range(4):
                 if n < PAIR:
                     regroup_x(nc.vector.tensor_copy, x_first[which], n, which)
                 else:
-                    regroup_x(gpsimd_copy, x_second[which], n, which)
-        for bunch in range(BUNCHES):
-            flip_weights(weights_now, bunch)
+                    regroup_x(nc.scalar.copy, x_second[which], n, which)
         for which in range(4):
             quantise_x(x_first[which], 0, which)
         for bunch in range(BUNCHES):
@@ -272,7 +277,12 @@ def tile_modelnew_pa_kernel(tc, x, weight, bias, out):
             )
 
         n_units = O_TILES * PAIRS
-        SITES = 3
+        SITES = 4
+
+        def prepare_weights(w, step):
+            sort_weights(w, step)
+            quantise_weights(w, step - 2)
+            flip_weights(w, step - 1)
 
         def completed_o_tile(index):
             if 0 <= index < n_units and index % PAIRS == PAIRS - 1:
@@ -291,7 +301,7 @@ def tile_modelnew_pa_kernel(tc, x, weight, bias, out):
                 if pair == 0:
                     if o_tile > 0:
                         weights_now = weights_next
-                    weights_next = sort_weights(o_tile + 1) if o_tile + 1 < O_TILES else None
+                    weights_next = new_weights(o_tile + 1) if o_tile + 1 < O_TILES else None
                     batch_tiles.append(
                         {
                             "six_m": batches.tile([P, PAIRS * COLS], F32, name="six_m"),
@@ -316,14 +326,14 @@ def tile_modelnew_pa_kernel(tc, x, weight, bias, out):
                 weights_next = None
             now = unit_or_none(i)
             before = unit_or_none(i - 1)
-            bunch = pair * SITES
+            step = pair * SITES
 
             centre_tap(now)
             cross_tap(now, 1, 2, seed=True)
+            prepare_weights(weights_next, step)
             fold_corner(now, 2, 2, seed=True)
             cross_tap(now, 2, 1)
-            quantise_weights(weights_next, bunch - 1)
-            flip_weights(weights_next, bunch)
+            prepare_weights(weights_next, step + 1)
             folded_20 = fold_corner(now, 2, 0)
 
             relu_smallest(before)
@@ -336,13 +346,11 @@ def tile_modelnew_pa_kernel(tc, x, weight, bias, out):
             best_of_extremes(before)
             cross_tap(now, 1, 0)
             merge_corners(before)
-            quantise_weights(weights_next, bunch)
-            flip_weights(weights_next, bunch + 1)
+            prepare_weights(weights_next, step + 2)
             folded_02 = fold_corner(now, 0, 2)
             cross_tap(now, 0, 1)
             clip(before)
-            quantise_weights(weights_next, bunch + 1)
-            flip_weights(weights_next, bunch + 2)
+            prepare_weights(weights_next, step + 3)
             folded_00 = fold_corner(now, 0, 0)
             corner_max(now, folded_20, 2, 0)
             hardswish_times_six(before)

@@ -57,7 +57,7 @@ def tile_modelnew_pa_kernel(tc, x, weight, bias, out):
         w_stage = stack.enter_context(tc.tile_pool(name="w_stage", bufs=2))
         w_ready = stack.enter_context(tc.tile_pool(name="w_ready", bufs=2))
         stats = stack.enter_context(tc.tile_pool(name="stats", bufs=3))
-        batches = stack.enter_context(tc.tile_pool(name="batches", bufs=3))
+        late = stack.enter_context(tc.tile_pool(name="late", bufs=6))
         psum = stack.enter_context(tc.psum_pool(name="psum", bufs=6))
         psum_w = stack.enter_context(tc.psum_pool(name="psum_w", bufs=2))
         stack.enter_context(tc.manual_schedule())
@@ -86,11 +86,6 @@ def tile_modelnew_pa_kernel(tc, x, weight, bias, out):
         bias_bf = keep.tile([P, O_TILES], BF16, name="bias_bf")
         with nc.allow_non_contiguous_dma(reason="512 bias values, one to a partition and o-tile"):
             nc.scalar.dma_start(out=bias_bf, in_=bias.rearrange("(k p) -> p k", p=P))
-
-        bias_t = keep.tile([P, O_TILES], F32, name="bias_t")
-        bias_t3 = keep.tile([P, O_TILES], F32, name="bias_t3")
-        nc.vector.tensor_scalar_add(out=bias_t, in0=bias_bf, scalar1=-0.5)
-        nc.vector.tensor_scalar_add(out=bias_t3, in0=bias_bf, scalar1=2.5)
 
         def new_weights(o_tile):
             by_tap = w_stage.tile([P, TAPS, C_IN], BF16, name="w_by_tap")
@@ -165,16 +160,29 @@ def tile_modelnew_pa_kernel(tc, x, weight, bias, out):
         for bunch in range(BUNCHES):
             flip_weights(weights_now, bunch)
         x_first, x_second = new_x_tiles(), new_x_tiles()
-        for n in range(IMAGES):
+        for n in range(PAIR):
             for which in range(4):
-                if n < PAIR:
-                    regroup_x(nc.vector.tensor_copy, x_first[which], n, which)
-                else:
-                    regroup_x(nc.scalar.copy, x_second[which], n, which)
+                regroup_x(nc.vector.tensor_copy, x_first[which], n, which)
         for which in range(4):
             quantise_x(x_first[which], 0, which)
         for bunch in range(BUNCHES):
             quantise_weights(weights_now, bunch)
+
+        bias_t = keep.tile([P, O_TILES], F32, name="bias_t")
+        bias_t3 = keep.tile([P, O_TILES], F32, name="bias_t3")
+        nc.vector.tensor_scalar_add(out=bias_t, in0=bias_bf, scalar1=-0.5)
+        nc.vector.tensor_scalar_add(out=bias_t3, in0=bias_bf, scalar1=2.5)
+
+        def prepare_second_pair(step):
+            if step < 4:
+                for n in range(PAIR, IMAGES):
+                    regroup_x(nc.scalar.copy, x_second[step], n, step)
+            if 1 <= step <= 4:
+                quantise_x(x_second[step - 1], 1, step - 1)
+
+        EARLY_X_STEPS = 2
+        for step in range(EARLY_X_STEPS):
+            prepare_second_pair(step)
 
         def tap_sums(unit, kh, kw):
             which = 2 * tap_geometry(kh)[1] + tap_geometry(kw)[1]
@@ -191,14 +199,14 @@ def tile_modelnew_pa_kernel(tc, x, weight, bias, out):
             )
             return sums
 
-        def centre_tap(unit):
+        def seed_extremes(unit, kh, kw):
             if unit is None:
                 return
             nc.scalar.activation(
-                out=unit["largest"], in_=tap_sums(unit, 1, 1), func=ACT.Identity, bias=unit["bias_t"], scale=1.0
+                out=unit["largest"], in_=tap_sums(unit, kh, kw), func=ACT.Identity, bias=unit["bias_t"], scale=1.0
             )
 
-        def cross_tap(unit, kh, kw, seed=False):
+        def extremes_tap(unit, kh, kw, seed=False):
             if unit is None:
                 return
             source = tap_source(tap_sums(unit, kh, kw), kh, kw)
@@ -212,20 +220,23 @@ def tile_modelnew_pa_kernel(tc, x, weight, bias, out):
                 in1=tap_target(unit["largest"], kh, kw), op0=ALU.add, op1=ALU.max,
             )
 
-        def fold_corner(unit, kh, kw, seed=False):
+        def fold_relu(unit, kh, kw, seed=False):
             if unit is None:
                 return None
-            folded = unit["corner"] if seed else stats.tile([P, COLS], F32, name="folded", bufs=5)
+            folded = unit["folded"] if seed else stats.tile([P, COLS], F32, name="fold", bufs=6)
             nc.scalar.activation(
                 out=folded, in_=tap_sums(unit, kh, kw), func=ACT.Relu, bias=unit["bias_t3"], scale=1.0
             )
-            nc.scalar.activation(out=folded, in_=folded, func=ACT.Abs, bias=-1.5, scale=1.0)
             return folded
 
-        def corner_max(unit, folded, kh, kw):
+        def fold_abs(folded):
+            if folded is not None:
+                nc.scalar.activation(out=folded, in_=folded, func=ACT.Abs, bias=-1.5, scale=1.0)
+
+        def fold_max(unit, folded, kh, kw):
             if unit is None:
                 return
-            target = tap_target(unit["corner"], kh, kw)
+            target = tap_target(unit["folded"], kh, kw)
             nc.vector.tensor_tensor(out=target, in0=tap_source(folded, kh, kw), in1=target, op=ALU.max)
 
         def relu_smallest(unit):
@@ -239,10 +250,10 @@ def tile_modelnew_pa_kernel(tc, x, weight, bias, out):
                     op0=ALU.mult, op1=ALU.max,
                 )
 
-        def merge_corners(unit):
+        def merge_folded(unit):
             if unit is not None:
                 nc.vector.scalar_tensor_tensor(
-                    out=unit["largest"], in0=unit["corner"], scalar=-1.5, in1=unit["largest"],
+                    out=unit["largest"], in0=unit["folded"], scalar=-1.5, in1=unit["largest"],
                     op0=ALU.add, op1=ALU.max,
                 )
 
@@ -266,15 +277,17 @@ def tile_modelnew_pa_kernel(tc, x, weight, bias, out):
             if unit is not None:
                 nc.scalar.activation(out=unit["gate"], in_=unit["gate"], func=ACT.Exp)
 
-        def finish(o_tile, batch):
+        def log_gate(unit):
+            nc.scalar.activation(out=unit["gate"], in_=unit["gate"], func=ACT.Ln, bias=1.0, scale=1.0)
+
+        def tanh_gate(unit):
+            nc.scalar.activation(out=unit["gate"], in_=unit["gate"], func=ACT.Tanh)
+
+        def finish(unit):
             nc.vector.scalar_tensor_tensor(
-                out=batch["gate"], in0=batch["six_m"], scalar=1.0 / 6.0, in1=batch["gate"],
-                op0=ALU.mult, op1=ALU.mult,
+                out=unit["gate"], in0=unit["six_m"], scalar=1.0 / 6.0, in1=unit["gate"], op0=ALU.mult, op1=ALU.mult
             )
-            nc.sync.dma_start(
-                out=out[:, o_tile * P : (o_tile + 1) * P].rearrange("n o a b -> o n (a b)"),
-                in_=batch["gate"].rearrange("p (n x) -> p n x", n=IMAGES),
-            )
+            nc.sync.dma_start(out=unit["out"], in_=unit["gate"].rearrange("p (i x) -> p i x", i=PAIR))
 
         n_units = O_TILES * PAIRS
         SITES = 4
@@ -284,16 +297,15 @@ def tile_modelnew_pa_kernel(tc, x, weight, bias, out):
             quantise_weights(w, step - 2)
             flip_weights(w, step - 1)
 
-        def completed_o_tile(index):
+        def o_tile_completed_by(index):
             if 0 <= index < n_units and index % PAIRS == PAIRS - 1:
-                return index // PAIRS
-            return None
+                return units[index - PAIRS + 1 : index + 1]
+            return []
 
         def unit_or_none(index):
             return units[index] if 0 <= index < len(units) else None
 
         units = []
-        batch_tiles = []
         weights_next = None
         for i in range(n_units + 3):
             o_tile, pair = divmod(i, PAIRS)
@@ -302,24 +314,21 @@ def tile_modelnew_pa_kernel(tc, x, weight, bias, out):
                     if o_tile > 0:
                         weights_now = weights_next
                     weights_next = new_weights(o_tile + 1) if o_tile + 1 < O_TILES else None
-                    batch_tiles.append(
-                        {
-                            "six_m": batches.tile([P, PAIRS * COLS], F32, name="six_m"),
-                            "gate": batches.tile([P, PAIRS * COLS], F32, name="gate"),
-                        }
-                    )
                 units.append(
                     {
                         "pair": pair,
+                        "out": out[pair * PAIR : (pair + 1) * PAIR, o_tile * P : (o_tile + 1) * P].rearrange(
+                            "i o a b -> o i (a b)"
+                        ),
                         "codes": weights_now["codes"],
                         "scales": weights_now["scales"],
                         "bias_t": bias_t[:, o_tile : o_tile + 1],
                         "bias_t3": bias_t3[:, o_tile : o_tile + 1],
                         "largest": stats.tile([P, COLS], F32, name="largest"),
                         "smallest": stats.tile([P, COLS], F32, name="smallest"),
-                        "corner": stats.tile([P, COLS], F32, name="corner"),
-                        "six_m": batch_tiles[o_tile]["six_m"][:, pair * COLS : (pair + 1) * COLS],
-                        "gate": batch_tiles[o_tile]["gate"][:, pair * COLS : (pair + 1) * COLS],
+                        "folded": stats.tile([P, COLS], F32, name="folded"),
+                        "six_m": late.tile([P, COLS], F32, name="six_m"),
+                        "gate": late.tile([P, COLS], F32, name="gate"),
                     }
                 )
             else:
@@ -327,42 +336,46 @@ def tile_modelnew_pa_kernel(tc, x, weight, bias, out):
             now = unit_or_none(i)
             before = unit_or_none(i - 1)
             step = pair * SITES
+            x_step = EARLY_X_STEPS + i * (SITES + 1)
 
-            centre_tap(now)
-            cross_tap(now, 1, 2, seed=True)
+            seed_extremes(now, 1, 1)
+            fold_22 = fold_relu(now, 2, 2, seed=True)
+            extremes_tap(now, 1, 2, seed=True)
             prepare_weights(weights_next, step)
-            fold_corner(now, 2, 2, seed=True)
-            cross_tap(now, 2, 1)
-            prepare_weights(weights_next, step + 1)
-            folded_20 = fold_corner(now, 2, 0)
+            prepare_second_pair(x_step)
+            fold_20 = fold_relu(now, 2, 0)
+            fold_abs(fold_22)
 
             relu_smallest(before)
-            closing = completed_o_tile(i - 3)
-            if closing is not None:
-                gate = batch_tiles[closing]["gate"]
-                nc.scalar.activation(out=gate, in_=gate, func=ACT.Tanh)
+            fold_abs(fold_20)
+            for unit in o_tile_completed_by(i - 3):
+                tanh_gate(unit)
             exp_gate(unit_or_none(i - 2))
 
+            extremes_tap(now, 2, 1)
             best_of_extremes(before)
-            cross_tap(now, 1, 0)
-            merge_corners(before)
+            prepare_weights(weights_next, step + 1)
+            prepare_second_pair(x_step + 1)
+            extremes_tap(now, 1, 0)
+            merge_folded(before)
             prepare_weights(weights_next, step + 2)
-            folded_02 = fold_corner(now, 0, 2)
-            cross_tap(now, 0, 1)
+            prepare_second_pair(x_step + 2)
+            fold_02 = fold_relu(now, 0, 2)
+            extremes_tap(now, 0, 1)
             clip(before)
-            prepare_weights(weights_next, step + 3)
-            folded_00 = fold_corner(now, 0, 0)
-            corner_max(now, folded_20, 2, 0)
+            fold_00 = fold_relu(now, 0, 0)
+            fold_abs(fold_02)
+            fold_max(now, fold_20, 2, 0)
             hardswish_times_six(before)
-            corner_max(now, folded_02, 0, 2)
+            prepare_weights(weights_next, step + 3)
+            prepare_second_pair(x_step + 3)
+            fold_abs(fold_00)
+            fold_max(now, fold_02, 0, 2)
             cap(before)
-            corner_max(now, folded_00, 0, 0)
+            fold_max(now, fold_00, 0, 0)
+            prepare_second_pair(x_step + 4)
 
-            if i == 0:
-                for which in range(4):
-                    quantise_x(x_second[which], 1, which)
-            if completed_o_tile(i - 2) is not None:
-                gate = batch_tiles[completed_o_tile(i - 2)]["gate"]
-                nc.scalar.activation(out=gate, in_=gate, func=ACT.Ln, bias=1.0, scale=1.0)
-            if closing is not None:
-                finish(closing, batch_tiles[closing])
+            for unit in o_tile_completed_by(i - 2):
+                log_gate(unit)
+            for unit in o_tile_completed_by(i - 3):
+                finish(unit)

@@ -225,13 +225,15 @@ def tile_modelnew_pa_kernel(tc, x, weight, bias, out):
                 return None
             folded = unit["folded"] if seed else stats.tile([P, COLS], F32, name="fold", bufs=6)
             nc.scalar.activation(
-                out=folded, in_=tap_sums(unit, kh, kw), func=ACT.Relu, bias=unit["bias_t3"], scale=1.0
+                out=tap_source(folded, kh, kw), in_=tap_source(tap_sums(unit, kh, kw), kh, kw),
+                func=ACT.Relu, bias=unit["bias_t3"], scale=1.0,
             )
             return folded
 
-        def fold_abs(folded):
+        def fold_abs(folded, kh, kw):
             if folded is not None:
-                nc.scalar.activation(out=folded, in_=folded, func=ACT.Abs, bias=-1.5, scale=1.0)
+                used = tap_source(folded, kh, kw)
+                nc.scalar.activation(out=used, in_=used, func=ACT.Abs, bias=-1.5, scale=1.0)
 
         def fold_max(unit, folded, kh, kw):
             if unit is None:
@@ -344,10 +346,10 @@ def tile_modelnew_pa_kernel(tc, x, weight, bias, out):
             prepare_weights(weights_next, step)
             prepare_second_pair(x_step)
             fold_20 = fold_relu(now, 2, 0)
-            fold_abs(fold_22)
+            fold_abs(fold_22, 2, 2)
 
             relu_smallest(before)
-            fold_abs(fold_20)
+            fold_abs(fold_20, 2, 0)
             for unit in o_tile_completed_by(i - 3):
                 tanh_gate(unit)
             exp_gate(unit_or_none(i - 2))
@@ -364,12 +366,12 @@ def tile_modelnew_pa_kernel(tc, x, weight, bias, out):
             extremes_tap(now, 0, 1)
             clip(before)
             fold_00 = fold_relu(now, 0, 0)
-            fold_abs(fold_02)
+            fold_abs(fold_02, 0, 2)
             fold_max(now, fold_20, 2, 0)
             hardswish_times_six(before)
             prepare_weights(weights_next, step + 3)
             prepare_second_pair(x_step + 3)
-            fold_abs(fold_00)
+            fold_abs(fold_00, 0, 0)
             fold_max(now, fold_02, 0, 2)
             cap(before)
             fold_max(now, fold_00, 0, 0)

@@ -76,10 +76,7 @@ def tile_modelnew_pa_kernel(tc, x, weight, bias, out):
 
         load_weights(0)
         for n in range(IMAGES):
-            nc.sync.dma_start(
-                out=x_raw[n].rearrange("q (u e) s -> q u (e s)", u=HALVES),
-                in_=x[n].rearrange("(u q e) h w -> q u (e h w)", u=HALVES, q=P),
-            )
+            nc.sync.dma_start(out=x_raw[n], in_=x[n].rearrange("(q j) h w -> q j (h w)", j=PACK))
         for o_tile in range(1, O_TILES):
             load_weights(o_tile)
 
@@ -88,11 +85,13 @@ def tile_modelnew_pa_kernel(tc, x, weight, bias, out):
             nc.scalar.dma_start(out=bias_bf, in_=bias.rearrange("(k p) -> p k", p=P))
 
         def new_weights(o_tile):
-            by_tap = w_stage.tile([P, TAPS, C_IN], BF16, name="w_by_tap")
+            blocks = w_stage.tile([P, SORT_GROUPS, P, SORT_GROUP, PACK], BF16, name="w_sorted")
             return {
-                "rows": w_rows[o_tile].rearrange("o (c t) -> o c t", t=TAPS),
-                "by_tap": by_tap,
-                "by_tap_words": by_tap.rearrange("o t c -> o (t c)").bitcast(F32),
+                "rows": w_rows[o_tile].rearrange("o (q j t) -> o q j t", j=PACK, t=TAPS),
+                "sorted": blocks,
+                "sorted_words": blocks.rearrange("o g q i j -> o (g q i j)")
+                .bitcast(F32)
+                .rearrange("o (g q i u) -> o g q i u", g=SORT_GROUPS, q=P, u=HALVES),
                 "grouped": w_stage.tile([P, TAPS, P * PACK], BF16, name="w_grouped", align_bytes=64),
                 "codes": w_ready.tile([P, TAPS, P], U32, name="w_codes", align_bytes=64),
                 "scales": w_ready.tile([P, TAPS, P], U8, name="w_scales", align_bytes=64),
@@ -103,7 +102,8 @@ def tile_modelnew_pa_kernel(tc, x, weight, bias, out):
                 return
             t0, t1 = group * SORT_GROUP, min((group + 1) * SORT_GROUP, TAPS)
             nc.vector.tensor_copy(
-                out=w["by_tap"][:, t0:t1, :].rearrange("o t c -> o c t"), in_=w["rows"][:, :, t0:t1]
+                out=w["sorted"][:, group, :, 0 : t1 - t0, :].rearrange("o q i j -> o q j i"),
+                in_=w["rows"][:, :, :, t0:t1],
             )
 
         def flip_weights(w, bunch):
@@ -113,8 +113,9 @@ def tile_modelnew_pa_kernel(tc, x, weight, bias, out):
             flipped = psum_w.tile([P, BUNCH, HALVES, P], F32, name="flipped")
             for t in range(t0, t1):
                 for u in range(HALVES):
-                    first_word = (t * HALVES + u) * P
-                    nc.tensor.transpose(flipped[:, t - t0, u, :], w["by_tap_words"][:, first_word : first_word + P], identity)
+                    nc.tensor.transpose(
+                        flipped[:, t - t0, u, :], w["sorted_words"][:, t // SORT_GROUP, :, t % SORT_GROUP, u], identity
+                    )
             words = w["grouped"][:, t0:t1, :].rearrange("q t k -> q (t k)").bitcast(F32)
             nc.scalar.copy(
                 out=words.rearrange("q (t o u) -> q t o u", t=t1 - t0, u=HALVES),
@@ -271,13 +272,11 @@ def tile_modelnew_pa_kernel(tc, x, weight, bias, out):
 
         def cap(unit):
             if unit is not None:
-                nc.vector.tensor_scalar(
-                    out=unit["gate"], in0=unit["six_m"], scalar1=1.0 / 6.0, scalar2=EXP_CAP, op0=ALU.mult, op1=ALU.min
-                )
+                nc.scalar.activation(out=unit["gate"], in_=unit["six_m"], func=ACT.Relu, bias=EXP_CAP, scale=-1.0 / 6.0)
 
         def exp_gate(unit):
             if unit is not None:
-                nc.scalar.activation(out=unit["gate"], in_=unit["gate"], func=ACT.Exp)
+                nc.scalar.activation(out=unit["gate"], in_=unit["gate"], func=ACT.Exp, bias=EXP_CAP, scale=-1.0)
 
         def log_gate(unit):
             nc.scalar.activation(out=unit["gate"], in_=unit["gate"], func=ACT.Ln, bias=1.0, scale=1.0)
@@ -349,6 +348,7 @@ def tile_modelnew_pa_kernel(tc, x, weight, bias, out):
             fold_abs(fold_22, 2, 2)
 
             relu_smallest(before)
+            cap(unit_or_none(i - 2))
             fold_abs(fold_20, 2, 0)
             for unit in o_tile_completed_by(i - 3):
                 tanh_gate(unit)
@@ -373,7 +373,6 @@ def tile_modelnew_pa_kernel(tc, x, weight, bias, out):
             prepare_second_pair(x_step + 3)
             fold_abs(fold_00, 0, 0)
             fold_max(now, fold_02, 0, 2)
-            cap(before)
             fold_max(now, fold_00, 0, 0)
             prepare_second_pair(x_step + 4)
 

@@ -29,6 +29,31 @@ SORT_GROUP = 4
 SORT_GROUPS = (TAPS + SORT_GROUP - 1) // SORT_GROUP
 EXP_CAP = 20.0
 
+CENTRE = (1, 1)
+ALL_TAPS = [(1, 1), (1, 2), (2, 1), (1, 0), (0, 1), (0, 2), (2, 0), (0, 0), (2, 2)]
+FOLD_TAPS = [(2, 2), (0, 0), (2, 0), (0, 2), (0, 1), (1, 0)]
+FOLD_TILES = 6
+SORT_LEAD = 3
+FIRST_BUNCHES = 3
+BUNCH_ORDER = [2, 4, 0, 3, 1]
+BATCH_LAST = (5, 7)
+LOG_TURN, TANH_TURN = 2, 3
+FOLDS_BY_TURN = (4, 5, 5, 5, 5, 5, 4, 2)
+EARLY_X_CLASSES = 2
+
+
+def fold_count(i):
+    return FOLDS_BY_TURN[i]
+
+
+def batch_of(units, last):
+    first = 0
+    for other in BATCH_LAST:
+        if other < last:
+            first = other + 1
+    return units[first : last + 1]
+
+
 FLOPS = 2 * TAPS * IMAGES * OUT_PIXELS * C_OUT * C_IN
 
 
@@ -57,7 +82,7 @@ def tile_modelnew_pa_kernel(tc, x, weight, bias, out):
         w_stage = stack.enter_context(tc.tile_pool(name="w_stage", bufs=2))
         w_ready = stack.enter_context(tc.tile_pool(name="w_ready", bufs=2))
         stats = stack.enter_context(tc.tile_pool(name="stats", bufs=3))
-        late = stack.enter_context(tc.tile_pool(name="late", bufs=6))
+        late = stack.enter_context(tc.tile_pool(name="late", bufs=8))
         psum = stack.enter_context(tc.psum_pool(name="psum", bufs=6))
         psum_w = stack.enter_context(tc.psum_pool(name="psum_w", bufs=2))
         stack.enter_context(tc.manual_schedule())
@@ -85,21 +110,17 @@ def tile_modelnew_pa_kernel(tc, x, weight, bias, out):
             nc.scalar.dma_start(out=bias_bf, in_=bias.rearrange("(k p) -> p k", p=P))
 
         def new_weights(o_tile):
-            blocks = w_stage.tile([P, SORT_GROUPS, P, SORT_GROUP, PACK], BF16, name="w_sorted")
-            return {
-                "rows": w_rows[o_tile].rearrange("o (q j t) -> o q j t", j=PACK, t=TAPS),
-                "sorted": blocks,
-                "sorted_words": blocks.rearrange("o g q i j -> o (g q i j)")
-                .bitcast(F32)
-                .rearrange("o (g q i u) -> o g q i u", g=SORT_GROUPS, q=P, u=HALVES),
-                "grouped": w_stage.tile([P, TAPS, P * PACK], BF16, name="w_grouped", align_bytes=64),
-                "codes": w_ready.tile([P, TAPS, P], U32, name="w_codes", align_bytes=64),
-                "scales": w_ready.tile([P, TAPS, P], U8, name="w_scales", align_bytes=64),
-            }
+            return {"rows": w_rows[o_tile].rearrange("o (q j t) -> o q j t", j=PACK, t=TAPS)}
 
         def sort_weights(w, group):
-            if w is None or group < 0 or group >= SORT_GROUPS:
-                return
+            if group == 0:
+                blocks = w_stage.tile([P, SORT_GROUPS, P, SORT_GROUP, PACK], BF16, name="w_sorted")
+                w["sorted"] = blocks
+                w["sorted_words"] = (
+                    blocks.rearrange("o g q i j -> o (g q i j)")
+                    .bitcast(F32)
+                    .rearrange("o (g q i u) -> o g q i u", g=SORT_GROUPS, q=P, u=HALVES)
+                )
             t0, t1 = group * SORT_GROUP, min((group + 1) * SORT_GROUP, TAPS)
             nc.vector.tensor_copy(
                 out=w["sorted"][:, group, :, 0 : t1 - t0, :].rearrange("o q i j -> o q j i"),
@@ -107,8 +128,8 @@ def tile_modelnew_pa_kernel(tc, x, weight, bias, out):
             )
 
         def flip_weights(w, bunch):
-            if w is None or bunch < 0 or bunch >= BUNCHES:
-                return
+            if "grouped" not in w:
+                w["grouped"] = w_stage.tile([P, TAPS, P * PACK], BF16, name="w_grouped", align_bytes=64)
             t0, t1 = bunch * BUNCH, min((bunch + 1) * BUNCH, TAPS)
             flipped = psum_w.tile([P, BUNCH, HALVES, P], F32, name="flipped")
             for t in range(t0, t1):
@@ -123,8 +144,9 @@ def tile_modelnew_pa_kernel(tc, x, weight, bias, out):
             )
 
         def quantise_weights(w, bunch):
-            if w is None or bunch < 0 or bunch >= BUNCHES:
-                return
+            if "codes" not in w:
+                w["codes"] = w_ready.tile([P, TAPS, P], U32, name="w_codes", align_bytes=64)
+                w["scales"] = w_ready.tile([P, TAPS, P], U8, name="w_scales", align_bytes=64)
             t0, t1 = bunch * BUNCH, min((bunch + 1) * BUNCH, TAPS)
             nc.vector.quantize_mx(
                 out=w["codes"][:, t0:t1, :].rearrange("q t o -> q (t o)").bitcast(FP8X4),
@@ -155,11 +177,11 @@ def tile_modelnew_pa_kernel(tc, x, weight, bias, out):
                 for which in range(4)
             ]
 
-        weights_now = new_weights(0)
+        weights = [new_weights(o_tile) for o_tile in range(O_TILES)]
         for group in range(SORT_GROUPS):
-            sort_weights(weights_now, group)
+            sort_weights(weights[0], group)
         for bunch in range(BUNCHES):
-            flip_weights(weights_now, bunch)
+            flip_weights(weights[0], bunch)
         x_first, x_second = new_x_tiles(), new_x_tiles()
         for n in range(PAIR):
             for which in range(4):
@@ -167,32 +189,29 @@ def tile_modelnew_pa_kernel(tc, x, weight, bias, out):
         for which in range(4):
             quantise_x(x_first[which], 0, which)
         for bunch in range(BUNCHES):
-            quantise_weights(weights_now, bunch)
+            quantise_weights(weights[0], bunch)
 
         bias_t = keep.tile([P, O_TILES], F32, name="bias_t")
         bias_t3 = keep.tile([P, O_TILES], F32, name="bias_t3")
         nc.vector.tensor_scalar_add(out=bias_t, in0=bias_bf, scalar1=-0.5)
         nc.vector.tensor_scalar_add(out=bias_t3, in0=bias_bf, scalar1=2.5)
 
-        def prepare_second_pair(step):
-            if step < 4:
-                for n in range(PAIR, IMAGES):
-                    regroup_x(nc.scalar.copy, x_second[step], n, step)
-            if 1 <= step <= 4:
-                quantise_x(x_second[step - 1], 1, step - 1)
+        for group in range(SORT_GROUPS):
+            sort_weights(weights[1], group)
 
-        EARLY_X_STEPS = 2
-        for step in range(EARLY_X_STEPS):
-            prepare_second_pair(step)
+        for which in range(EARLY_X_CLASSES):
+            for n in range(PAIR, IMAGES):
+                regroup_x(nc.scalar.copy, x_second[which], n, which)
 
-        def tap_sums(unit, kh, kw):
+        def tap_sums(unit, tap):
+            kh, kw = tap
             which = 2 * tap_geometry(kh)[1] + tap_geometry(kw)[1]
             t = kh * KERNEL + kw
             sums = psum.tile([P, COLS], F32, name="sums")
             nc.tensor.matmul_mx(
                 out=sums,
-                lhsT=unit["codes"][:, t, :].bitcast(FP8X4),
-                lhsT_scale=unit["scales"][:, t, :],
+                lhsT=unit["weights"]["codes"][:, t, :].bitcast(FP8X4),
+                lhsT_scale=unit["weights"]["scales"][:, t, :],
                 rhs=x_codes[:, unit["pair"], which, :].bitcast(FP8X4),
                 rhs_scale=x_scales[:, unit["pair"], which, :],
                 start=True,
@@ -200,18 +219,15 @@ def tile_modelnew_pa_kernel(tc, x, weight, bias, out):
             )
             return sums
 
-        def seed_extremes(unit, kh, kw):
-            if unit is None:
-                return
+        def seed_extremes(unit):
             nc.scalar.activation(
-                out=unit["largest"], in_=tap_sums(unit, kh, kw), func=ACT.Identity, bias=unit["bias_t"], scale=1.0
+                out=unit["largest"], in_=tap_sums(unit, CENTRE), func=ACT.Identity, bias=unit["bias_t"], scale=1.0
             )
 
-        def extremes_tap(unit, kh, kw, seed=False):
-            if unit is None:
-                return
-            source = tap_source(tap_sums(unit, kh, kw), kh, kw)
-            low = unit["largest"] if seed else unit["smallest"]
+        def extremes_tap(unit, tap, first):
+            kh, kw = tap
+            source = tap_source(tap_sums(unit, tap), kh, kw)
+            low = unit["largest"] if first else unit["smallest"]
             nc.vector.scalar_tensor_tensor(
                 out=tap_target(unit["smallest"], kh, kw), in0=source, scalar=unit["bias_t"],
                 in1=tap_target(low, kh, kw), op0=ALU.add, op1=ALU.min,
@@ -221,62 +237,51 @@ def tile_modelnew_pa_kernel(tc, x, weight, bias, out):
                 in1=tap_target(unit["largest"], kh, kw), op0=ALU.add, op1=ALU.max,
             )
 
-        def fold_relu(unit, kh, kw, seed=False):
-            if unit is None:
-                return None
-            folded = unit["folded"] if seed else stats.tile([P, COLS], F32, name="fold", bufs=6)
+        def fold_relu(unit, tap, first):
+            kh, kw = tap
+            folded = unit["folded"] if first else stats.tile([P, COLS], F32, name="fold", bufs=FOLD_TILES)
             nc.scalar.activation(
-                out=tap_source(folded, kh, kw), in_=tap_source(tap_sums(unit, kh, kw), kh, kw),
+                out=tap_source(folded, kh, kw), in_=tap_source(tap_sums(unit, tap), kh, kw),
                 func=ACT.Relu, bias=unit["bias_t3"], scale=1.0,
             )
             return folded
 
-        def fold_abs(folded, kh, kw):
-            if folded is not None:
-                used = tap_source(folded, kh, kw)
-                nc.scalar.activation(out=used, in_=used, func=ACT.Abs, bias=-1.5, scale=1.0)
+        def fold_abs(folded, tap):
+            used = tap_source(folded, tap[0], tap[1])
+            nc.scalar.activation(out=used, in_=used, func=ACT.Abs, bias=-1.5, scale=1.0)
 
-        def fold_max(unit, folded, kh, kw):
-            if unit is None:
-                return
-            target = tap_target(unit["folded"], kh, kw)
-            nc.vector.tensor_tensor(out=target, in0=tap_source(folded, kh, kw), in1=target, op=ALU.max)
+        def fold_max(unit, folded, tap):
+            target = tap_target(unit["folded"], tap[0], tap[1])
+            nc.vector.tensor_tensor(out=target, in0=tap_source(folded, tap[0], tap[1]), in1=target, op=ALU.max)
 
         def relu_smallest(unit):
-            if unit is not None:
-                nc.scalar.activation(out=unit["smallest"], in_=unit["smallest"], func=ACT.Relu, bias=3.0, scale=1.0)
+            nc.vector.tensor_scalar(
+                out=unit["smallest"], in0=unit["smallest"], scalar1=3.0, scalar2=0.0, op0=ALU.add, op1=ALU.max
+            )
 
         def best_of_extremes(unit):
-            if unit is not None:
-                nc.vector.scalar_tensor_tensor(
-                    out=unit["largest"], in0=unit["smallest"], scalar=-1.0, in1=unit["largest"],
-                    op0=ALU.mult, op1=ALU.max,
-                )
+            nc.vector.scalar_tensor_tensor(
+                out=unit["largest"], in0=unit["smallest"], scalar=-1.0, in1=unit["largest"], op0=ALU.mult, op1=ALU.max
+            )
 
         def merge_folded(unit):
-            if unit is not None:
-                nc.vector.scalar_tensor_tensor(
-                    out=unit["largest"], in0=unit["folded"], scalar=-1.5, in1=unit["largest"],
-                    op0=ALU.add, op1=ALU.max,
-                )
+            nc.vector.scalar_tensor_tensor(
+                out=unit["largest"], in0=unit["folded"], scalar=-1.5, in1=unit["largest"], op0=ALU.add, op1=ALU.max
+            )
 
         def clip(unit):
-            if unit is not None:
-                nc.vector.tensor_scalar(
-                    out=unit["smallest"], in0=unit["largest"], scalar1=3.0, scalar2=6.0, op0=ALU.add, op1=ALU.min
-                )
+            nc.vector.tensor_scalar(
+                out=unit["smallest"], in0=unit["largest"], scalar1=3.0, scalar2=6.0, op0=ALU.add, op1=ALU.min
+            )
 
-        def hardswish_times_six(unit):
-            if unit is not None:
-                nc.vector.tensor_tensor(out=unit["six_m"], in0=unit["largest"], in1=unit["smallest"], op=ALU.mult)
+        def hardswish_times_six(unit, engine):
+            engine.tensor_tensor(out=unit["six_m"], in0=unit["largest"], in1=unit["smallest"], op=ALU.mult)
 
         def cap(unit):
-            if unit is not None:
-                nc.scalar.activation(out=unit["gate"], in_=unit["six_m"], func=ACT.Relu, bias=EXP_CAP, scale=-1.0 / 6.0)
+            nc.scalar.activation(out=unit["gate"], in_=unit["six_m"], func=ACT.Relu, bias=EXP_CAP, scale=-1.0 / 6.0)
 
         def exp_gate(unit):
-            if unit is not None:
-                nc.scalar.activation(out=unit["gate"], in_=unit["gate"], func=ACT.Exp, bias=EXP_CAP, scale=-1.0)
+            nc.scalar.activation(out=unit["gate"], in_=unit["gate"], func=ACT.Exp, bias=EXP_CAP, scale=-1.0)
 
         def log_gate(unit):
             nc.scalar.activation(out=unit["gate"], in_=unit["gate"], func=ACT.Ln, bias=1.0, scale=1.0)
@@ -291,92 +296,103 @@ def tile_modelnew_pa_kernel(tc, x, weight, bias, out):
             nc.sync.dma_start(out=unit["out"], in_=unit["gate"].rearrange("p (i x) -> p i x", i=PAIR))
 
         n_units = O_TILES * PAIRS
-        SITES = 4
-
-        def prepare_weights(w, step):
-            sort_weights(w, step)
-            quantise_weights(w, step - 2)
-            flip_weights(w, step - 1)
-
-        def o_tile_completed_by(index):
-            if 0 <= index < n_units and index % PAIRS == PAIRS - 1:
-                return units[index - PAIRS + 1 : index + 1]
-            return []
-
-        def unit_or_none(index):
-            return units[index] if 0 <= index < len(units) else None
-
         units = []
-        weights_next = None
-        for i in range(n_units + 3):
+
+        def new_unit(i):
             o_tile, pair = divmod(i, PAIRS)
+            return {
+                "pair": pair,
+                "out": out[pair * PAIR : (pair + 1) * PAIR, o_tile * P : (o_tile + 1) * P].rearrange("i o a b -> o i (a b)"),
+                "weights": weights[o_tile],
+                "bias_t": bias_t[:, o_tile : o_tile + 1],
+                "bias_t3": bias_t3[:, o_tile : o_tile + 1],
+                "largest": stats.tile([P, COLS], F32, name="largest"),
+                "smallest": stats.tile([P, COLS], F32, name="smallest"),
+                "folded": stats.tile([P, COLS], F32, name="folded"),
+                "six_m": late.tile([P, COLS], F32, name="six_m"),
+                "gate": late.tile([P, COLS], F32, name="gate"),
+            }
+
+        def call(step):
+            step[0](*step[1:])
+
+        for i in range(n_units + 2):
+            now = None
             if i < n_units:
-                if pair == 0:
-                    if o_tile > 0:
-                        weights_now = weights_next
-                    weights_next = new_weights(o_tile + 1) if o_tile + 1 < O_TILES else None
-                units.append(
-                    {
-                        "pair": pair,
-                        "out": out[pair * PAIR : (pair + 1) * PAIR, o_tile * P : (o_tile + 1) * P].rearrange(
-                            "i o a b -> o i (a b)"
-                        ),
-                        "codes": weights_now["codes"],
-                        "scales": weights_now["scales"],
-                        "bias_t": bias_t[:, o_tile : o_tile + 1],
-                        "bias_t3": bias_t3[:, o_tile : o_tile + 1],
-                        "largest": stats.tile([P, COLS], F32, name="largest"),
-                        "smallest": stats.tile([P, COLS], F32, name="smallest"),
-                        "folded": stats.tile([P, COLS], F32, name="folded"),
-                        "six_m": late.tile([P, COLS], F32, name="six_m"),
-                        "gate": late.tile([P, COLS], F32, name="gate"),
-                    }
-                )
-            else:
-                weights_next = None
-            now = unit_or_none(i)
-            before = unit_or_none(i - 1)
-            step = pair * SITES
-            x_step = EARLY_X_STEPS + i * (SITES + 1)
+                now = new_unit(i)
+                units.append(now)
+            before = units[i - 1] if 1 <= i <= n_units else None
 
-            seed_extremes(now, 1, 1)
-            fold_22 = fold_relu(now, 2, 2, seed=True)
-            extremes_tap(now, 1, 2, seed=True)
-            prepare_weights(weights_next, step)
-            prepare_second_pair(x_step)
-            fold_20 = fold_relu(now, 2, 0)
-            fold_abs(fold_22, 2, 2)
+            scalar_jobs, vector_jobs = [], []
+            for o_tile in range(1, O_TILES):
+                lead = o_tile * PAIRS - i
+                if lead == SORT_LEAD:
+                    vector_jobs += [(sort_weights, weights[o_tile], group) for group in range(SORT_GROUPS)]
+                bunches = []
+                if lead == 2:
+                    bunches = BUNCH_ORDER[:FIRST_BUNCHES]
+                if lead == 1:
+                    bunches = BUNCH_ORDER[FIRST_BUNCHES:]
+                scalar_jobs += [(flip_weights, weights[o_tile], bunch) for bunch in bunches]
+                vector_jobs += [(quantise_weights, weights[o_tile], bunch) for bunch in bunches]
+            if i == 0:
+                for which in range(4):
+                    if which >= EARLY_X_CLASSES:
+                        for n in range(PAIR, IMAGES):
+                            scalar_jobs.append((regroup_x, nc.scalar.copy, x_second[which], n, which))
+                    vector_jobs.append((quantise_x, x_second[which], 1, which))
+            logs = [unit for last in BATCH_LAST if i == last + LOG_TURN for unit in batch_of(units, last)]
+            tanhs = [unit for last in BATCH_LAST if i == min(last + TANH_TURN, n_units + 1) for unit in batch_of(units, last)]
+            scalar_fill = [(log_gate, unit) for unit in logs]
+            vector_jobs += [(finish, unit) for unit in tanhs]
 
-            relu_smallest(before)
-            cap(unit_or_none(i - 2))
-            fold_abs(fold_20, 2, 0)
-            for unit in o_tile_completed_by(i - 3):
+            folds = FOLD_TAPS[: fold_count(i)] if now is not None else []
+            extremes = [tap for tap in ALL_TAPS if tap != CENTRE and tap not in folds] if now is not None else []
+
+            if now is not None:
+                seed_extremes(now)
+            fold_tiles = []
+            for position in range(max(len(folds), len(extremes))):
+                if position < len(folds):
+                    fold_tiles.append(fold_relu(now, folds[position], position == 0))
+                    if position >= 1:
+                        fold_abs(fold_tiles[position - 1], folds[position - 1])
+                if position < len(extremes):
+                    extremes_tap(now, extremes[position], position == 0)
+                if scalar_fill:
+                    call(scalar_fill[0])
+                    scalar_fill = scalar_fill[1:]
+                elif scalar_jobs and position % 2 == 1:
+                    call(scalar_jobs[0])
+                    scalar_jobs = scalar_jobs[1:]
+            if folds:
+                fold_abs(fold_tiles[-1], folds[-1])
+            for step in scalar_fill:
+                call(step)
+            for unit in tanhs:
                 tanh_gate(unit)
-            exp_gate(unit_or_none(i - 2))
+            if before is not None:
+                cap(before)
+            for step in scalar_jobs[:1]:
+                call(step)
+            if before is not None:
+                exp_gate(before)
+            for step in scalar_jobs[1:]:
+                call(step)
 
-            extremes_tap(now, 2, 1)
-            best_of_extremes(before)
-            prepare_weights(weights_next, step + 1)
-            prepare_second_pair(x_step + 1)
-            extremes_tap(now, 1, 0)
-            merge_folded(before)
-            prepare_weights(weights_next, step + 2)
-            prepare_second_pair(x_step + 2)
-            fold_02 = fold_relu(now, 0, 2)
-            extremes_tap(now, 0, 1)
-            clip(before)
-            fold_00 = fold_relu(now, 0, 0)
-            fold_abs(fold_02, 0, 2)
-            fold_max(now, fold_20, 2, 0)
-            hardswish_times_six(before)
-            prepare_weights(weights_next, step + 3)
-            prepare_second_pair(x_step + 3)
-            fold_abs(fold_00, 0, 0)
-            fold_max(now, fold_02, 0, 2)
-            fold_max(now, fold_00, 0, 0)
-            prepare_second_pair(x_step + 4)
-
-            for unit in o_tile_completed_by(i - 2):
-                log_gate(unit)
-            for unit in o_tile_completed_by(i - 3):
-                finish(unit)
+            chain, between = [], []
+            if now is not None:
+                chain = [(fold_max, now, fold_tiles[k], folds[k]) for k in range(1, len(folds))]
+                chain += [(merge_folded, now), (clip, now)]
+                between = [(relu_smallest, now), (best_of_extremes, now)]
+            room = max(len(chain) - len(between), 0)
+            first_jobs = max(len(vector_jobs) - room, 0)
+            for step in vector_jobs[:first_jobs]:
+                call(step)
+            between += vector_jobs[first_jobs:]
+            for k in range(len(chain)):
+                if k < len(between):
+                    call(between[k])
+                call(chain[k])
+            if now is not None:
+                hardswish_times_six(now, nc.gpsimd if i < n_units - 1 else nc.vector)

@@ -33,12 +33,12 @@ CENTRE = (1, 1)
 ALL_TAPS = [(1, 1), (1, 2), (2, 1), (1, 0), (0, 1), (0, 2), (2, 0), (0, 0), (2, 2)]
 FOLD_TAPS = [(2, 2), (0, 0), (2, 0), (0, 2), (0, 1), (1, 0)]
 FOLD_TILES = 6
-SORT_LEAD = 3
-FIRST_BUNCHES = 3
+SORTS_BY_LEAD = {4: [1, 2], 3: [0]}
+FIRST_BUNCHES = 2
 BUNCH_ORDER = [2, 4, 0, 3, 1]
 BATCH_LAST = (5, 7)
 LOG_TURN, TANH_TURN = 2, 3
-FOLDS_BY_TURN = (4, 5, 5, 5, 5, 5, 4, 2)
+FOLDS_BY_TURN = (4, 4, 4, 4, 4, 5, 4, 2)
 EARLY_X_CLASSES = 2
 
 
@@ -112,8 +112,8 @@ def tile_modelnew_pa_kernel(tc, x, weight, bias, out):
         def new_weights(o_tile):
             return {"rows": w_rows[o_tile].rearrange("o (q j t) -> o q j t", j=PACK, t=TAPS)}
 
-        def sort_weights(w, group):
-            if group == 0:
+        def sort_weights(w, group, on_gpsimd=False):
+            if "sorted" not in w:
                 blocks = w_stage.tile([P, SORT_GROUPS, P, SORT_GROUP, PACK], BF16, name="w_sorted")
                 w["sorted"] = blocks
                 w["sorted_words"] = (
@@ -122,10 +122,17 @@ def tile_modelnew_pa_kernel(tc, x, weight, bias, out):
                     .rearrange("o (g q i u) -> o g q i u", g=SORT_GROUPS, q=P, u=HALVES)
                 )
             t0, t1 = group * SORT_GROUP, min((group + 1) * SORT_GROUP, TAPS)
-            nc.vector.tensor_copy(
-                out=w["sorted"][:, group, :, 0 : t1 - t0, :].rearrange("o q i j -> o q j i"),
-                in_=w["rows"][:, :, :, t0:t1],
-            )
+            if on_gpsimd:
+                nc.gpsimd.tensor_scalar(
+                    out=w["sorted"][:, group, :, 0 : t1 - t0, :],
+                    in0=w["rows"][:, :, :, t0:t1].rearrange("o q j i -> o q i j"),
+                    scalar1=1.0, scalar2=0.0, op0=ALU.mult, op1=ALU.add,
+                )
+            else:
+                nc.vector.tensor_copy(
+                    out=w["sorted"][:, group, :, 0 : t1 - t0, :].rearrange("o q i j -> o q j i"),
+                    in_=w["rows"][:, :, :, t0:t1],
+                )
 
         def flip_weights(w, bunch):
             if "grouped" not in w:
@@ -323,11 +330,10 @@ def tile_modelnew_pa_kernel(tc, x, weight, bias, out):
                 units.append(now)
             before = units[i - 1] if 1 <= i <= n_units else None
 
-            scalar_jobs, vector_jobs = [], []
+            scalar_jobs, vector_jobs, gpsimd_jobs = [], [], []
             for o_tile in range(1, O_TILES):
                 lead = o_tile * PAIRS - i
-                if lead == SORT_LEAD:
-                    vector_jobs += [(sort_weights, weights[o_tile], group) for group in range(SORT_GROUPS)]
+                gpsimd_jobs += [(sort_weights, weights[o_tile], group, True) for group in SORTS_BY_LEAD.get(lead, [])]
                 bunches = []
                 if lead == 2:
                     bunches = BUNCH_ORDER[:FIRST_BUNCHES]
@@ -396,3 +402,5 @@ def tile_modelnew_pa_kernel(tc, x, weight, bias, out):
                 call(chain[k])
             if now is not None:
                 hardswish_times_six(now, nc.gpsimd if i < n_units - 1 else nc.vector)
+            for step in gpsimd_jobs:
+                call(step)

@@ -30,8 +30,9 @@ SORT_GROUPS = (TAPS + SORT_GROUP - 1) // SORT_GROUP
 EXP_CAP = 20.0
 
 CENTRE = (1, 1)
-ALL_TAPS = [(1, 1), (1, 2), (2, 1), (1, 0), (0, 1), (0, 2), (2, 0), (0, 0), (2, 2)]
-FOLD_TAPS = [(2, 2), (0, 0), (2, 0), (0, 2), (0, 1), (1, 0)]
+LEFT_SEED = (2, 0)
+ALL_TAPS = [(1, 1), (1, 2), (2, 1), (0, 1), (0, 2), (1, 0), (2, 0), (0, 0), (2, 2)]
+FOLD_TAPS = [(2, 2), (0, 0), (2, 0), (1, 0), (0, 2), (0, 1)]
 FOLD_TILES = 6
 SORTS_BY_LEAD = {4: [1, 2], 3: [0]}
 FIRST_BUNCHES = 2
@@ -72,6 +73,14 @@ def tap_source(sums, kh, kw):
 
 def tap_target(running, kh, kw):
     return as_images(running)[:, :, -tap_geometry(kh)[0] : OUT_SIDE, -tap_geometry(kw)[0] : OUT_SIDE]
+
+
+def used_rows(flat, kh):
+    return as_images(flat)[:, :, 0 : OUT_SIDE + tap_geometry(kh)[0], :]
+
+
+def target_rows(flat, kh):
+    return as_images(flat)[:, :, -tap_geometry(kh)[0] : OUT_SIDE, :]
 
 
 def tile_modelnew_pa_kernel(tc, x, weight, bias, out):
@@ -248,18 +257,22 @@ def tile_modelnew_pa_kernel(tc, x, weight, bias, out):
             kh, kw = tap
             folded = unit["folded"] if first else stats.tile([P, COLS], F32, name="fold", bufs=FOLD_TILES)
             nc.scalar.activation(
-                out=tap_source(folded, kh, kw), in_=tap_source(tap_sums(unit, tap), kh, kw),
+                out=used_rows(folded, kh), in_=used_rows(tap_sums(unit, tap), kh),
                 func=ACT.Relu, bias=unit["bias_t3"], scale=1.0,
             )
             return folded
 
         def fold_abs(folded, tap):
-            used = tap_source(folded, tap[0], tap[1])
+            used = used_rows(folded, tap[0])
             nc.scalar.activation(out=used, in_=used, func=ACT.Abs, bias=-1.5, scale=1.0)
 
         def fold_max(unit, folded, tap):
             target = tap_target(unit["folded"], tap[0], tap[1])
             nc.vector.tensor_tensor(out=target, in0=tap_source(folded, tap[0], tap[1]), in1=target, op=ALU.max)
+
+        def fold_max_left(left, folded, tap):
+            target = target_rows(left, tap[0])
+            nc.vector.tensor_tensor(out=target, in0=used_rows(folded, tap[0]), in1=target, op=ALU.max)
 
         def relu_smallest(unit):
             nc.vector.tensor_scalar(
@@ -388,7 +401,16 @@ def tile_modelnew_pa_kernel(tc, x, weight, bias, out):
 
             chain, between = [], []
             if now is not None:
-                chain = [(fold_max, now, fold_tiles[k], folds[k]) for k in range(1, len(folds))]
+                if LEFT_SEED in folds:
+                    left = fold_tiles[folds.index(LEFT_SEED)]
+                    chain = [
+                        (fold_max_left, left, fold_tiles[k], folds[k])
+                        for k in range(1, len(folds)) if folds[k][1] == 0 and folds[k] != LEFT_SEED
+                    ]
+                    chain += [(fold_max, now, fold_tiles[k], folds[k]) for k in range(1, len(folds)) if folds[k][1] != 0]
+                    chain += [(fold_max, now, left, LEFT_SEED)]
+                else:
+                    chain = [(fold_max, now, fold_tiles[k], folds[k]) for k in range(1, len(folds))]
                 chain += [(merge_folded, now), (clip, now)]
                 between = [(relu_smallest, now), (best_of_extremes, now)]
             room = max(len(chain) - len(between), 0)

@@ -413,15 +413,18 @@ def tile_modelnew_pa_kernel(tc, x, weight, bias, out):
                     chain = [(fold_max, now, fold_tiles[k], folds[k]) for k in range(1, len(folds))]
                 chain += [(merge_folded, now), (clip, now)]
                 between = [(relu_smallest, now), (best_of_extremes, now)]
-            room = max(len(chain) - len(between), 0)
+            if 0 < len(chain) < 4:
+                call(between[0])
+                between = between[1:]
+            room = max(len(chain) - 1 - len(between), 0)
             first_jobs = max(len(vector_jobs) - room, 0)
             for step in vector_jobs[:first_jobs]:
                 call(step)
             between += vector_jobs[first_jobs:]
             for k in range(len(chain)):
+                call(chain[k])
                 if k < len(between):
                     call(between[k])
-                call(chain[k])
             if now is not None:
                 hardswish_times_six(now, nc.gpsimd if i < n_units - 1 else nc.vector)
             for step in gpsimd_jobs:

@@ -41,6 +41,7 @@ BATCH_LAST = (5, 7)
 LOG_TURN, TANH_TURN = 2, 3
 FOLDS_BY_TURN = (4, 4, 4, 4, 4, 5, 4, 2)
 EARLY_X_CLASSES = 2
+X_CLASS_ORDER = (0, 3, 1, 2)
 
 
 def fold_count(i):
@@ -215,7 +216,7 @@ def tile_modelnew_pa_kernel(tc, x, weight, bias, out):
         for group in range(SORT_GROUPS):
             sort_weights(weights[1], group)
 
-        for which in range(EARLY_X_CLASSES):
+        for which in X_CLASS_ORDER[:EARLY_X_CLASSES]:
             for n in range(PAIR, IMAGES):
                 regroup_x(nc.scalar.copy, x_second[which], n, which)
 
@@ -355,11 +356,10 @@ def tile_modelnew_pa_kernel(tc, x, weight, bias, out):
                 scalar_jobs += [(flip_weights, weights[o_tile], bunch) for bunch in bunches]
                 vector_jobs += [(quantise_weights, weights[o_tile], bunch) for bunch in bunches]
             if i == 0:
-                for which in range(4):
-                    if which >= EARLY_X_CLASSES:
-                        for n in range(PAIR, IMAGES):
-                            scalar_jobs.append((regroup_x, nc.scalar.copy, x_second[which], n, which))
-                    vector_jobs.append((quantise_x, x_second[which], 1, which))
+                for which in X_CLASS_ORDER[EARLY_X_CLASSES:]:
+                    for n in range(PAIR, IMAGES):
+                        scalar_jobs.append((regroup_x, nc.scalar.copy, x_second[which], n, which))
+                vector_jobs += [(quantise_x, x_second[which], 1, which) for which in X_CLASS_ORDER]
             logs = [unit for last in BATCH_LAST if i == last + LOG_TURN for unit in batch_of(units, last)]
             tanhs = [unit for last in BATCH_LAST if i == min(last + TANH_TURN, n_units + 1) for unit in batch_of(units, last)]
             scalar_fill = [(log_gate, unit) for unit in logs]

@@ -39,8 +39,9 @@ FIRST_BUNCHES = 2
 BUNCH_ORDER = [2, 4, 0, 3, 1]
 BATCH_LAST = (5, 7)
 LOG_TURN, TANH_TURN = 2, 3
-FOLDS_BY_TURN = (4, 4, 4, 4, 4, 5, 4, 2)
+FOLDS_BY_TURN = (3, 4, 4, 4, 4, 5, 4, 2)
 EARLY_X_CLASSES = 2
+VECTOR_LATE_CLASSES = ()
 X_CLASS_ORDER = (0, 3, 1, 2)
 
 
@@ -213,8 +214,8 @@ def tile_modelnew_pa_kernel(tc, x, weight, bias, out):
         nc.vector.tensor_scalar_add(out=bias_t, in0=bias_bf, scalar1=-0.5)
         nc.vector.tensor_scalar_add(out=bias_t3, in0=bias_bf, scalar1=2.5)
 
-        for group in range(SORT_GROUPS):
-            sort_weights(weights[1], group)
+        for group in (1, 2, 0):
+            sort_weights(weights[1], group, True)
 
         for which in X_CLASS_ORDER[:EARLY_X_CLASSES]:
             for n in range(PAIR, IMAGES):
@@ -344,7 +345,7 @@ def tile_modelnew_pa_kernel(tc, x, weight, bias, out):
                 units.append(now)
             before = units[i - 1] if 1 <= i <= n_units else None
 
-            scalar_jobs, vector_jobs, gpsimd_jobs = [], [], []
+            scalar_jobs, vector_jobs, gpsimd_jobs, late_flips = [], [], [], []
             for o_tile in range(1, O_TILES):
                 lead = o_tile * PAIRS - i
                 gpsimd_jobs += [(sort_weights, weights[o_tile], group, True) for group in SORTS_BY_LEAD.get(lead, [])]
@@ -353,12 +354,20 @@ def tile_modelnew_pa_kernel(tc, x, weight, bias, out):
                     bunches = BUNCH_ORDER[:FIRST_BUNCHES]
                 if lead == 1:
                     bunches = BUNCH_ORDER[FIRST_BUNCHES:]
+                if o_tile == 1 and lead == 2:
+                    late_flips += [(flip_weights, weights[o_tile], bunch) for bunch in bunches]
+                    continue
+                if o_tile == 1 and lead == 1:
+                    vector_jobs += [(quantise_weights, weights[o_tile], bunch) for bunch in BUNCH_ORDER[:FIRST_BUNCHES]]
                 scalar_jobs += [(flip_weights, weights[o_tile], bunch) for bunch in bunches]
                 vector_jobs += [(quantise_weights, weights[o_tile], bunch) for bunch in bunches]
             if i == 0:
                 for which in X_CLASS_ORDER[EARLY_X_CLASSES:]:
                     for n in range(PAIR, IMAGES):
-                        scalar_jobs.append((regroup_x, nc.scalar.copy, x_second[which], n, which))
+                        if which in VECTOR_LATE_CLASSES:
+                            vector_jobs.append((regroup_x, nc.vector.tensor_copy, x_second[which], n, which))
+                        else:
+                            scalar_jobs.append((regroup_x, nc.scalar.copy, x_second[which], n, which))
                 vector_jobs += [(quantise_x, x_second[which], 1, which) for which in X_CLASS_ORDER]
             logs = [unit for last in BATCH_LAST if i == last + LOG_TURN for unit in batch_of(units, last)]
             tanhs = [unit for last in BATCH_LAST if i == min(last + TANH_TURN, n_units + 1) for unit in batch_of(units, last)]
@@ -396,7 +405,7 @@ def tile_modelnew_pa_kernel(tc, x, weight, bias, out):
                 call(step)
             if before is not None:
                 exp_gate(before)
-            for step in scalar_jobs[1:]:
+            for step in scalar_jobs[1:] + late_flips:
                 call(step)
 
             chain, between = [], []

@@ -41,6 +41,7 @@ BATCH_LAST = (5, 7)
 LOG_TURN, TANH_TURN = 2, 3
 FOLDS_BY_TURN = (3, 4, 4, 4, 4, 5, 4, 2)
 EARLY_X_CLASSES = 2
+NEAR = 4
 VECTOR_LATE_CLASSES = ()
 X_CLASS_ORDER = (0, 3, 1, 2)
 
@@ -176,9 +177,9 @@ def tile_modelnew_pa_kernel(tc, x, weight, bias, out):
         x_scales = keep.tile([P, PAIRS, 4, COLS], U8, name="x_scales", align_bytes=64)
 
         def regroup_x(copy, grouped, n, which):
-            by_parity = x_raw[n].rearrange("p j (a r b s) -> p r s a b j", r=2, b=OUT_SIDE, s=2)
+            by_parity = x_raw[n].rearrange("p j (a r b i s) -> p r s a b j i", r=2, b=OUT_SIDE // NEAR, i=NEAR, s=2)
             copy(
-                out=grouped[:, n % PAIR].rearrange("p (a b) j -> p a b j", b=OUT_SIDE),
+                out=grouped[:, n % PAIR].rearrange("p (a b i) j -> p a b j i", b=OUT_SIDE // NEAR, i=NEAR),
                 in_=by_parity[:, which // 2, which % 2],
             )
 

@@ -27,7 +27,7 @@ BUNCH = 2
 BUNCHES = (TAPS + BUNCH - 1) // BUNCH
 SORT_GROUP = 4
 SORT_GROUPS = (TAPS + SORT_GROUP - 1) // SORT_GROUP
-EXP_CAP = 20.0
+LOG_FLOOR = 1e-18
 
 CENTRE = (1, 1)
 LEFT_SEED = (2, 0)
@@ -36,13 +36,18 @@ FOLD_TAPS = [(2, 2), (0, 0), (2, 0), (1, 0), (0, 2), (0, 1)]
 FOLD_TILES = 6
 SORTS_BY_LEAD = {4: [1, 2], 3: [0]}
 FIRST_BUNCHES = 2
+FLIP_BANKS = 2
+FLIP_POSITION = 0
+JOB_POSITION = 3
 BUNCH_ORDER = [2, 4, 0, 3, 1]
-BATCH_LAST = (5, 7)
+BATCH_LAST = (5,)
 LOG_TURN, TANH_TURN = 2, 3
-FOLDS_BY_TURN = (3, 4, 4, 4, 4, 5, 4, 2)
+FOLDS_BY_TURN = (2, 4, 4, 4, 4, 5, 4, 4)
 EARLY_X_CLASSES = 2
+VECTOR_LATE_CLASSES = 2
 NEAR = 4
-VECTOR_LATE_CLASSES = ()
+FIRST_PARTS = 2
+FIRST_BUNCH_ORDER = (2, 3, 4, 0, 1)
 X_CLASS_ORDER = (0, 3, 1, 2)
 
 
@@ -68,6 +73,10 @@ def tap_geometry(k):
 
 def as_images(flat):
     return flat.rearrange("p (i a b) -> p i a b", i=PAIR, a=OUT_SIDE)
+
+
+def image(flat, n):
+    return flat[:, n * OUT_PIXELS : (n + 1) * OUT_PIXELS]
 
 
 def tap_source(sums, kh, kw):
@@ -105,13 +114,16 @@ def tile_modelnew_pa_kernel(tc, x, weight, bias, out):
         w_rows = [keep.tile([P, C_IN * TAPS], BF16, name="w_rows%d" % o_tile) for o_tile in range(O_TILES)]
         x_raw = [keep.tile([P, PACK, SIDE * SIDE], BF16, name="x_raw%d" % n) for n in range(IMAGES)]
 
-        def load_weights(o_tile):
+        def load_weights(o_tile, part=0, parts=1):
+            width = C_IN * TAPS // parts
+            cols = slice(part * width, (part + 1) * width)
             nc.sync.dma_start(
-                out=w_rows[o_tile],
-                in_=weight[o_tile * P : (o_tile + 1) * P].rearrange("o c kh kw -> o (c kh kw)"),
+                out=w_rows[o_tile][:, cols],
+                in_=weight[o_tile * P : (o_tile + 1) * P].rearrange("o c kh kw -> o (c kh kw)")[:, cols],
             )
 
-        load_weights(0)
+        for part in range(FIRST_PARTS):
+            load_weights(0, part, FIRST_PARTS)
         for n in range(IMAGES):
             nc.sync.dma_start(out=x_raw[n], in_=x[n].rearrange("(q j) h w -> q j (h w)", j=PACK))
         for o_tile in range(1, O_TILES):
@@ -121,10 +133,13 @@ def tile_modelnew_pa_kernel(tc, x, weight, bias, out):
         with nc.allow_non_contiguous_dma(reason="512 bias values, one to a partition and o-tile"):
             nc.scalar.dma_start(out=bias_bf, in_=bias.rearrange("(k p) -> p k", p=P))
 
+        warm = keep.tile([P, 1], F32, name="warm")
+        nc.scalar.activation(out=warm, in_=identity[:, 0:1], func=ACT.Sigmoid)
+
         def new_weights(o_tile):
             return {"rows": w_rows[o_tile].rearrange("o (q j t) -> o q j t", j=PACK, t=TAPS)}
 
-        def sort_weights(w, group, on_gpsimd=False):
+        def sort_weights(w, group, on_gpsimd=False, part=0, parts=1):
             if "sorted" not in w:
                 blocks = w_stage.tile([P, SORT_GROUPS, P, SORT_GROUP, PACK], BF16, name="w_sorted")
                 w["sorted"] = blocks
@@ -134,6 +149,7 @@ def tile_modelnew_pa_kernel(tc, x, weight, bias, out):
                     .rearrange("o (g q i u) -> o g q i u", g=SORT_GROUPS, q=P, u=HALVES)
                 )
             t0, t1 = group * SORT_GROUP, min((group + 1) * SORT_GROUP, TAPS)
+            q = slice(part * P // parts, (part + 1) * P // parts)
             if on_gpsimd:
                 nc.gpsimd.tensor_scalar(
                     out=w["sorted"][:, group, :, 0 : t1 - t0, :],
@@ -142,20 +158,25 @@ def tile_modelnew_pa_kernel(tc, x, weight, bias, out):
                 )
             else:
                 nc.vector.tensor_copy(
-                    out=w["sorted"][:, group, :, 0 : t1 - t0, :].rearrange("o q i j -> o q j i"),
-                    in_=w["rows"][:, :, :, t0:t1],
+                    out=w["sorted"][:, group, q, 0 : t1 - t0, :].rearrange("o q i j -> o q j i"),
+                    in_=w["rows"][:, q, :, t0:t1],
                 )
 
-        def flip_weights(w, bunch):
-            if "grouped" not in w:
-                w["grouped"] = w_stage.tile([P, TAPS, P * PACK], BF16, name="w_grouped", align_bytes=64)
+        def transpose_weights(w, bunch):
             t0, t1 = bunch * BUNCH, min((bunch + 1) * BUNCH, TAPS)
             flipped = psum_w.tile([P, BUNCH, HALVES, P], F32, name="flipped")
+            w["flipped%d" % bunch] = flipped
             for t in range(t0, t1):
                 for u in range(HALVES):
                     nc.tensor.transpose(
                         flipped[:, t - t0, u, :], w["sorted_words"][:, t // SORT_GROUP, :, t % SORT_GROUP, u], identity
                     )
+
+        def copy_weights(w, bunch):
+            if "grouped" not in w:
+                w["grouped"] = w_stage.tile([P, TAPS, P * PACK], BF16, name="w_grouped", align_bytes=64)
+            t0, t1 = bunch * BUNCH, min((bunch + 1) * BUNCH, TAPS)
+            flipped = w["flipped%d" % bunch]
             words = w["grouped"][:, t0:t1, :].rearrange("q t k -> q (t k)").bitcast(F32)
             nc.scalar.copy(
                 out=words.rearrange("q (t o u) -> q t o u", t=t1 - t0, u=HALVES),
@@ -197,30 +218,33 @@ def tile_modelnew_pa_kernel(tc, x, weight, bias, out):
             ]
 
         weights = [new_weights(o_tile) for o_tile in range(O_TILES)]
-        for group in range(SORT_GROUPS):
-            sort_weights(weights[0], group)
-        for bunch in range(BUNCHES):
-            flip_weights(weights[0], bunch)
-        x_first, x_second = new_x_tiles(), new_x_tiles()
-        for n in range(PAIR):
-            for which in range(4):
-                regroup_x(nc.vector.tensor_copy, x_first[which], n, which)
-        for which in range(4):
-            quantise_x(x_first[which], 0, which)
-        for bunch in range(BUNCHES):
-            quantise_weights(weights[0], bunch)
-
+        for part in range(FIRST_PARTS):
+            for group in (1, 2, 0):
+                sort_weights(weights[0], group, False, part, FIRST_PARTS)
         bias_t = keep.tile([P, O_TILES], F32, name="bias_t")
         bias_t3 = keep.tile([P, O_TILES], F32, name="bias_t3")
         nc.vector.tensor_scalar_add(out=bias_t, in0=bias_bf, scalar1=-0.5)
         nc.vector.tensor_scalar_add(out=bias_t3, in0=bias_bf, scalar1=2.5)
 
+        for bunch in FIRST_BUNCH_ORDER:
+            transpose_weights(weights[0], bunch)
+            copy_weights(weights[0], bunch)
+        x_first, x_second = new_x_tiles(), new_x_tiles()
+        for which in range(4):
+            regroup_x(nc.vector.tensor_copy, x_first[which], 0, which)
+        for bunch in FIRST_BUNCH_ORDER:
+            quantise_weights(weights[0], bunch)
+        regroup_x(nc.vector.tensor_copy, x_first[0], 1, 0)
+        for which, then in ((1, 0), (3, 1), (2, 3)):
+            regroup_x(nc.vector.tensor_copy, x_first[which], 1, which)
+            quantise_x(x_first[then], 0, then)
+        quantise_x(x_first[2], 0, 2)
+
         for group in (1, 2, 0):
             sort_weights(weights[1], group, True)
 
         for which in X_CLASS_ORDER[:EARLY_X_CLASSES]:
-            for n in range(PAIR, IMAGES):
-                regroup_x(nc.scalar.copy, x_second[which], n, which)
+            regroup_x(nc.scalar.copy, x_second[which], PAIR, which)
 
         def tap_sums(unit, tap):
             kh, kw = tap
@@ -270,47 +294,71 @@ def tile_modelnew_pa_kernel(tc, x, weight, bias, out):
             nc.scalar.activation(out=used, in_=used, func=ACT.Abs, bias=-1.5, scale=1.0)
 
         def fold_max(unit, folded, tap):
-            target = tap_target(unit["folded"], tap[0], tap[1])
-            nc.vector.tensor_tensor(out=target, in0=tap_source(folded, tap[0], tap[1]), in1=target, op=ALU.max)
+            target, source = tap_target(unit["folded"], tap[0], tap[1]), tap_source(folded, tap[0], tap[1])
+            for n in range(PAIR):
+                nc.vector.tensor_tensor(out=target[:, n], in0=source[:, n], in1=target[:, n], op=ALU.max)
 
         def fold_max_left(left, folded, tap):
-            target = target_rows(left, tap[0])
-            nc.vector.tensor_tensor(out=target, in0=used_rows(folded, tap[0]), in1=target, op=ALU.max)
+            target, source = target_rows(left, tap[0]), used_rows(folded, tap[0])
+            for n in range(PAIR):
+                nc.vector.tensor_tensor(out=target[:, n], in0=source[:, n], in1=target[:, n], op=ALU.max)
 
         def relu_smallest(unit):
-            nc.vector.tensor_scalar(
-                out=unit["smallest"], in0=unit["smallest"], scalar1=3.0, scalar2=0.0, op0=ALU.add, op1=ALU.max
-            )
+            for n in range(PAIR):
+                smallest = image(unit["smallest"], n)
+                nc.vector.tensor_scalar(out=smallest, in0=smallest, scalar1=3.0, scalar2=0.0, op0=ALU.add, op1=ALU.max)
 
         def best_of_extremes(unit):
-            nc.vector.scalar_tensor_tensor(
-                out=unit["largest"], in0=unit["smallest"], scalar=-1.0, in1=unit["largest"], op0=ALU.mult, op1=ALU.max
-            )
+            for n in range(PAIR):
+                smallest, largest = image(unit["smallest"], n), image(unit["largest"], n)
+                nc.vector.scalar_tensor_tensor(
+                    out=largest, in0=smallest, scalar=-1.0, in1=largest, op0=ALU.mult, op1=ALU.max
+                )
 
         def merge_folded(unit):
-            nc.vector.scalar_tensor_tensor(
-                out=unit["largest"], in0=unit["folded"], scalar=-1.5, in1=unit["largest"], op0=ALU.add, op1=ALU.max
-            )
+            for n in range(PAIR):
+                folded, largest = image(unit["folded"], n), image(unit["largest"], n)
+                nc.vector.scalar_tensor_tensor(
+                    out=largest, in0=folded, scalar=-1.5, in1=largest, op0=ALU.add, op1=ALU.max
+                )
 
         def clip(unit):
-            nc.vector.tensor_scalar(
-                out=unit["smallest"], in0=unit["largest"], scalar1=3.0, scalar2=6.0, op0=ALU.add, op1=ALU.min
-            )
+            for n in range(PAIR):
+                nc.vector.tensor_scalar(
+                    out=image(unit["smallest"], n), in0=image(unit["largest"], n),
+                    scalar1=3.0, scalar2=6.0, op0=ALU.add, op1=ALU.min,
+                )
 
         def hardswish_times_six(unit, engine):
             engine.tensor_tensor(out=unit["six_m"], in0=unit["largest"], in1=unit["smallest"], op=ALU.mult)
 
-        def cap(unit):
-            nc.scalar.activation(out=unit["gate"], in_=unit["six_m"], func=ACT.Relu, bias=EXP_CAP, scale=-1.0 / 6.0)
-
-        def exp_gate(unit):
-            nc.scalar.activation(out=unit["gate"], in_=unit["gate"], func=ACT.Exp, bias=EXP_CAP, scale=-1.0)
+        def sigmoid_gate(unit):
+            nc.scalar.activation(out=unit["gate"], in_=unit["six_m"], func=ACT.Sigmoid, scale=-1.0 / 6.0)
 
         def log_gate(unit):
-            nc.scalar.activation(out=unit["gate"], in_=unit["gate"], func=ACT.Ln, bias=1.0, scale=1.0)
+            nc.scalar.activation(out=unit["gate"], in_=unit["gate"], func=ACT.Ln, bias=LOG_FLOOR, scale=1.0)
 
         def tanh_gate(unit):
-            nc.scalar.activation(out=unit["gate"], in_=unit["gate"], func=ACT.Tanh)
+            nc.scalar.activation(out=unit["gate"], in_=unit["gate"], func=ACT.Tanh, scale=-1.0)
+
+        def square_gate(unit):
+            for n in range(PAIR):
+                gate = image(unit["gate"], n)
+                nc.vector.tensor_tensor(out=gate, in0=gate, in1=gate, op=ALU.mult)
+
+        def widen_gate(unit):
+            for n in range(PAIR):
+                gate = image(unit["gate"], n)
+                nc.vector.scalar_tensor_tensor(out=gate, in0=gate, scalar=2.0, in1=gate, op0=ALU.add, op1=ALU.mult)
+
+        def root_gate(unit):
+            nc.scalar.activation(out=unit["gate"], in_=unit["gate"], func=ACT.Abs_reciprocal_sqrt, bias=9.0, scale=9.0)
+
+        def finish_root(unit):
+            nc.vector.scalar_tensor_tensor(
+                out=unit["gate"], in0=unit["gate"], scalar=-1.0 / 6.0, in1=unit["six_m"], op0=ALU.add, op1=ALU.mult
+            )
+            nc.sync.dma_start(out=unit["out"], in_=unit["gate"].rearrange("p (i x) -> p i x", i=PAIR))
 
         def finish(unit):
             nc.vector.scalar_tensor_tensor(
@@ -346,7 +394,7 @@ def tile_modelnew_pa_kernel(tc, x, weight, bias, out):
                 units.append(now)
             before = units[i - 1] if 1 <= i <= n_units else None
 
-            scalar_jobs, vector_jobs, gpsimd_jobs, late_flips = [], [], [], []
+            scalar_jobs, vector_jobs, gpsimd_jobs, late_flips, flips = [], [], [], [], []
             for o_tile in range(1, O_TILES):
                 lead = o_tile * PAIRS - i
                 gpsimd_jobs += [(sort_weights, weights[o_tile], group, True) for group in SORTS_BY_LEAD.get(lead, [])]
@@ -356,16 +404,17 @@ def tile_modelnew_pa_kernel(tc, x, weight, bias, out):
                 if lead == 1:
                     bunches = BUNCH_ORDER[FIRST_BUNCHES:]
                 if o_tile == 1 and lead == 2:
-                    late_flips += [(flip_weights, weights[o_tile], bunch) for bunch in bunches]
+                    late_flips += [(weights[o_tile], bunch) for bunch in bunches]
                     continue
                 if o_tile == 1 and lead == 1:
                     vector_jobs += [(quantise_weights, weights[o_tile], bunch) for bunch in BUNCH_ORDER[:FIRST_BUNCHES]]
-                scalar_jobs += [(flip_weights, weights[o_tile], bunch) for bunch in bunches]
+                flips += [(weights[o_tile], bunch) for bunch in bunches]
+                scalar_jobs += [(copy_weights, weights[o_tile], bunch) for bunch in bunches]
                 vector_jobs += [(quantise_weights, weights[o_tile], bunch) for bunch in bunches]
             if i == 0:
-                for which in X_CLASS_ORDER[EARLY_X_CLASSES:]:
-                    for n in range(PAIR, IMAGES):
-                        if which in VECTOR_LATE_CLASSES:
+                for k, which in enumerate(X_CLASS_ORDER):
+                    for n in range(PAIR + (1 if k < EARLY_X_CLASSES else 0), IMAGES):
+                        if n == IMAGES - 1 and k >= IMAGES - VECTOR_LATE_CLASSES:
                             vector_jobs.append((regroup_x, nc.vector.tensor_copy, x_second[which], n, which))
                         else:
                             scalar_jobs.append((regroup_x, nc.scalar.copy, x_second[which], n, which))
@@ -374,6 +423,10 @@ def tile_modelnew_pa_kernel(tc, x, weight, bias, out):
             tanhs = [unit for last in BATCH_LAST if i == min(last + TANH_TURN, n_units + 1) for unit in batch_of(units, last)]
             scalar_fill = [(log_gate, unit) for unit in logs]
             vector_jobs += [(finish, unit) for unit in tanhs]
+            if i == n_units:
+                vector_jobs = [(square_gate, units[-2]), (widen_gate, units[-2])] + vector_jobs + [(square_gate, units[-1]), (widen_gate, units[-1])]
+            if i == n_units + 1:
+                vector_jobs = [(finish_root, unit) for unit in units[-2:]]
 
             folds = FOLD_TAPS[: fold_count(i)] if now is not None else []
             extremes = [tap for tap in ALL_TAPS if tap != CENTRE and tap not in folds] if now is not None else []
@@ -382,32 +435,43 @@ def tile_modelnew_pa_kernel(tc, x, weight, bias, out):
                 seed_extremes(now)
             fold_tiles = []
             for position in range(max(len(folds), len(extremes))):
+                if i == 0 and position < len(extremes):
+                    extremes_tap(now, extremes[position], position == 0)
                 if position < len(folds):
                     fold_tiles.append(fold_relu(now, folds[position], position == 0))
                     if position >= 1:
                         fold_abs(fold_tiles[position - 1], folds[position - 1])
-                if position < len(extremes):
+                if i > 0 and position < len(extremes):
                     extremes_tap(now, extremes[position], position == 0)
+                if position == FLIP_POSITION:
+                    for flip in flips[:FLIP_BANKS]:
+                        transpose_weights(*flip)
                 if scalar_fill:
                     call(scalar_fill[0])
                     scalar_fill = scalar_fill[1:]
-                elif scalar_jobs and position % 2 == 1:
+                elif scalar_jobs and position >= JOB_POSITION and (position - JOB_POSITION) % 2 == 0:
                     call(scalar_jobs[0])
                     scalar_jobs = scalar_jobs[1:]
+            for flip in flips[FLIP_BANKS:]:
+                transpose_weights(*flip)
             if folds:
                 fold_abs(fold_tiles[-1], folds[-1])
             for step in scalar_fill:
                 call(step)
             for unit in tanhs:
                 tanh_gate(unit)
-            if before is not None:
-                cap(before)
+            if i == n_units + 1:
+                for unit in units[-2:]:
+                    root_gate(unit)
             for step in scalar_jobs[:1]:
                 call(step)
             if before is not None:
-                exp_gate(before)
-            for step in scalar_jobs[1:] + late_flips:
+                sigmoid_gate(before)
+            for step in scalar_jobs[1:]:
                 call(step)
+            for flip in late_flips:
+                transpose_weights(*flip)
+                copy_weights(*flip)
 
             chain, between = [], []
             if now is not None:

@@ -25,8 +25,6 @@ O_TILES = C_OUT // P
 HALVES = 2
 BUNCH = 2
 BUNCHES = (TAPS + BUNCH - 1) // BUNCH
-SORT_GROUP = 4
-SORT_GROUPS = (TAPS + SORT_GROUP - 1) // SORT_GROUP
 LOG_FLOOR = 1e-18
 
 CENTRE = (1, 1)
@@ -34,7 +32,7 @@ LEFT_SEED = (2, 0)
 ALL_TAPS = [(1, 1), (1, 2), (2, 1), (0, 1), (0, 2), (1, 0), (2, 0), (0, 0), (2, 2)]
 FOLD_TAPS = [(2, 2), (0, 0), (2, 0), (1, 0), (0, 2), (0, 1)]
 FOLD_TILES = 6
-SORTS_BY_LEAD = {4: [1, 2], 3: [0]}
+SORTS_BY_LEAD = {4: [2, 3], 3: [0, 1]}
 FIRST_BUNCHES = 2
 FLIP_BANKS = 2
 FLIP_POSITION = 0
@@ -137,30 +135,25 @@ def tile_modelnew_pa_kernel(tc, x, weight, bias, out):
         nc.scalar.activation(out=warm, in_=identity[:, 0:1], func=ACT.Sigmoid)
 
         def new_weights(o_tile):
-            return {"rows": w_rows[o_tile].rearrange("o (q j t) -> o q j t", j=PACK, t=TAPS)}
+            return {"rows": w_rows[o_tile].rearrange("o (c t) -> o c t", t=TAPS)}
 
-        def sort_weights(w, group, on_gpsimd=False, part=0, parts=1):
+        def sort_weights(w, bunch, engine="V", part=0, parts=1):
             if "sorted" not in w:
-                blocks = w_stage.tile([P, SORT_GROUPS, P, SORT_GROUP, PACK], BF16, name="w_sorted")
-                w["sorted"] = blocks
-                w["sorted_words"] = (
-                    blocks.rearrange("o g q i j -> o (g q i j)")
-                    .bitcast(F32)
-                    .rearrange("o (g q i u) -> o g q i u", g=SORT_GROUPS, q=P, u=HALVES)
-                )
-            t0, t1 = group * SORT_GROUP, min((group + 1) * SORT_GROUP, TAPS)
-            q = slice(part * P // parts, (part + 1) * P // parts)
-            if on_gpsimd:
+                by_tap = w_stage.tile([P, TAPS, C_IN], BF16, name="w_sorted")
+                w["sorted"] = by_tap
+                w["words"] = by_tap.rearrange("o t c -> o (t c)").bitcast(F32).rearrange("o (t q u) -> o t q u", t=TAPS, u=HALVES)
+            t0, t1 = bunch * BUNCH, min((bunch + 1) * BUNCH, TAPS)
+            c = slice(part * C_IN // parts, (part + 1) * C_IN // parts)
+            out_view = w["sorted"][:, t0:t1, c].rearrange("o t c -> o c t")
+            in_view = w["rows"][:, c, t0:t1]
+            if engine == "S":
+                nc.scalar.copy(out=out_view, in_=in_view)
+            elif engine == "G":
                 nc.gpsimd.tensor_scalar(
-                    out=w["sorted"][:, group, :, 0 : t1 - t0, :],
-                    in0=w["rows"][:, :, :, t0:t1].rearrange("o q j i -> o q i j"),
-                    scalar1=1.0, scalar2=0.0, op0=ALU.mult, op1=ALU.add,
+                    out=out_view, in0=in_view, scalar1=1.0, scalar2=0.0, op0=ALU.mult, op1=ALU.add
                 )
             else:
-                nc.vector.tensor_copy(
-                    out=w["sorted"][:, group, q, 0 : t1 - t0, :].rearrange("o q i j -> o q j i"),
-                    in_=w["rows"][:, q, :, t0:t1],
-                )
+                nc.vector.tensor_copy(out=out_view, in_=in_view)
 
         def transpose_weights(w, bunch):
             t0, t1 = bunch * BUNCH, min((bunch + 1) * BUNCH, TAPS)
@@ -169,7 +162,7 @@ def tile_modelnew_pa_kernel(tc, x, weight, bias, out):
             for t in range(t0, t1):
                 for u in range(HALVES):
                     nc.tensor.transpose(
-                        flipped[:, t - t0, u, :], w["sorted_words"][:, t // SORT_GROUP, :, t % SORT_GROUP, u], identity
+                        flipped[:, t - t0, u, :], w["words"][:, t, :, u], identity
                     )
 
         def copy_weights(w, bunch):
@@ -219,8 +212,8 @@ def tile_modelnew_pa_kernel(tc, x, weight, bias, out):
 
         weights = [new_weights(o_tile) for o_tile in range(O_TILES)]
         for part in range(FIRST_PARTS):
-            for group in (1, 2, 0):
-                sort_weights(weights[0], group, False, part, FIRST_PARTS)
+            for bunch in FIRST_BUNCH_ORDER:
+                sort_weights(weights[0], bunch, "V", part, FIRST_PARTS)
         bias_t = keep.tile([P, O_TILES], F32, name="bias_t")
         bias_t3 = keep.tile([P, O_TILES], F32, name="bias_t3")
         nc.vector.tensor_scalar_add(out=bias_t, in0=bias_bf, scalar1=-0.5)
@@ -240,8 +233,8 @@ def tile_modelnew_pa_kernel(tc, x, weight, bias, out):
             quantise_x(x_first[then], 0, then)
         quantise_x(x_first[2], 0, 2)
 
-        for group in (1, 2, 0):
-            sort_weights(weights[1], group, True)
+        for bunch in (2, 3, 0, 1):
+            sort_weights(weights[1], bunch, "G")
 
         for which in X_CLASS_ORDER[:EARLY_X_CLASSES]:
             regroup_x(nc.scalar.copy, x_second[which], PAIR, which)
@@ -397,7 +390,9 @@ def tile_modelnew_pa_kernel(tc, x, weight, bias, out):
             scalar_jobs, vector_jobs, gpsimd_jobs, late_flips, flips = [], [], [], [], []
             for o_tile in range(1, O_TILES):
                 lead = o_tile * PAIRS - i
-                gpsimd_jobs += [(sort_weights, weights[o_tile], group, True) for group in SORTS_BY_LEAD.get(lead, [])]
+                gpsimd_jobs += [(sort_weights, weights[o_tile], bunch, "G") for bunch in SORTS_BY_LEAD.get(lead, [])]
+                if lead == (2 if o_tile == 1 else 3):
+                    scalar_jobs.append((sort_weights, weights[o_tile], 4, "S"))
                 bunches = []
                 if lead == 2:
                     bunches = BUNCH_ORDER[:FIRST_BUNCHES]

@@ -37,10 +37,11 @@ FIRST_BUNCHES = 2
 FLIP_BANKS = 2
 FLIP_POSITION = 0
 JOB_POSITION = 3
+RELU_ON_SCALAR = (1,)
 BUNCH_ORDER = [2, 4, 0, 3, 1]
 BATCH_LAST = (5,)
 LOG_TURN, TANH_TURN = 2, 3
-FOLDS_BY_TURN = (2, 4, 4, 4, 4, 5, 4, 4)
+FOLDS_BY_TURN = (2, 4, 4, 4, 4, 6, 4, 4)
 EARLY_X_CLASSES = 2
 VECTOR_LATE_CLASSES = 2
 NEAR = 4
@@ -257,20 +258,20 @@ def tile_modelnew_pa_kernel(tc, x, weight, bias, out):
 
         def seed_extremes(unit):
             nc.scalar.activation(
-                out=unit["largest"], in_=tap_sums(unit, CENTRE), func=ACT.Identity, bias=unit["bias_t"], scale=1.0
+                out=unit["seed"], in_=tap_sums(unit, CENTRE), func=ACT.Identity, bias=unit["bias_t"], scale=1.0
             )
 
         def extremes_tap(unit, tap, first):
             kh, kw = tap
             source = tap_source(tap_sums(unit, tap), kh, kw)
-            low = unit["largest"] if first else unit["smallest"]
+            low, high = (unit["seed"], unit["seed"]) if first else (unit["smallest"], unit["largest"])
             nc.vector.scalar_tensor_tensor(
                 out=tap_target(unit["smallest"], kh, kw), in0=source, scalar=unit["bias_t"],
                 in1=tap_target(low, kh, kw), op0=ALU.add, op1=ALU.min,
             )
             nc.vector.scalar_tensor_tensor(
                 out=tap_target(unit["largest"], kh, kw), in0=source, scalar=unit["bias_t"],
-                in1=tap_target(unit["largest"], kh, kw), op0=ALU.add, op1=ALU.max,
+                in1=tap_target(high, kh, kw), op0=ALU.add, op1=ALU.max,
             )
 
         def fold_relu(unit, tap, first):
@@ -295,6 +296,9 @@ def tile_modelnew_pa_kernel(tc, x, weight, bias, out):
             target, source = target_rows(left, tap[0]), used_rows(folded, tap[0])
             for n in range(PAIR):
                 nc.vector.tensor_tensor(out=target[:, n], in0=source[:, n], in1=target[:, n], op=ALU.max)
+
+        def relu_smallest_scalar(unit):
+            nc.scalar.activation(out=unit["smallest"], in_=unit["smallest"], func=ACT.Relu, bias=3.0, scale=1.0)
 
         def relu_smallest(unit):
             for n in range(PAIR):
@@ -370,6 +374,7 @@ def tile_modelnew_pa_kernel(tc, x, weight, bias, out):
                 "weights": weights[o_tile],
                 "bias_t": bias_t[:, o_tile : o_tile + 1],
                 "bias_t3": bias_t3[:, o_tile : o_tile + 1],
+                "seed": stats.tile([P, COLS], F32, name="seed"),
                 "largest": stats.tile([P, COLS], F32, name="largest"),
                 "smallest": stats.tile([P, COLS], F32, name="smallest"),
                 "folded": stats.tile([P, COLS], F32, name="folded"),
@@ -460,6 +465,8 @@ def tile_modelnew_pa_kernel(tc, x, weight, bias, out):
                     root_gate(unit)
             for step in scalar_jobs[:1]:
                 call(step)
+            if now is not None and i in RELU_ON_SCALAR:
+                relu_smallest_scalar(now)
             if before is not None:
                 sigmoid_gate(before)
             for step in scalar_jobs[1:]:
@@ -480,9 +487,13 @@ def tile_modelnew_pa_kernel(tc, x, weight, bias, out):
                     chain += [(fold_max, now, left, LEFT_SEED)]
                 else:
                     chain = [(fold_max, now, fold_tiles[k], folds[k]) for k in range(1, len(folds))]
-                chain += [(merge_folded, now), (clip, now)]
-                between = [(relu_smallest, now), (best_of_extremes, now)]
-            if 0 < len(chain) < 4:
+                if i in RELU_ON_SCALAR:
+                    chain += [(merge_folded, now), (best_of_extremes, now), (clip, now)]
+                    between = []
+                else:
+                    chain += [(merge_folded, now), (clip, now)]
+                    between = [(relu_smallest, now), (best_of_extremes, now)]
+            if 0 < len(chain) < 4 and between:
                 call(between[0])
                 between = between[1:]
             room = max(len(chain) - 1 - len(between), 0)

@@ -32,16 +32,18 @@ LEFT_SEED = (2, 0)
 ALL_TAPS = [(1, 1), (1, 2), (2, 1), (0, 1), (0, 2), (1, 0), (2, 0), (0, 0), (2, 2)]
 FOLD_TAPS = [(2, 2), (0, 0), (2, 0), (1, 0), (0, 2), (0, 1)]
 FOLD_TILES = 6
-SORTS_BY_LEAD = {4: [2, 3], 3: [0, 1]}
+SORTS_BY_LEAD = {4: [2], 3: [0, 3], 2: [1]}
 FIRST_BUNCHES = 2
 FLIP_BANKS = 2
 FLIP_POSITION = 0
 JOB_POSITION = 3
-RELU_ON_SCALAR = (1,)
+X3_ON_GPSIMD = (2,)
+X1_ON_SCALAR = (3,)
+RELU_ON_SCALAR = (1, 2, 3)
 BUNCH_ORDER = [2, 4, 0, 3, 1]
 BATCH_LAST = (5,)
 LOG_TURN, TANH_TURN = 2, 3
-FOLDS_BY_TURN = (2, 4, 4, 4, 4, 6, 4, 4)
+FOLDS_BY_TURN = (2, 4, 4, 4, 4, 5, 4, 4)
 EARLY_X_CLASSES = 2
 VECTOR_LATE_CLASSES = 2
 NEAR = 4
@@ -123,14 +125,14 @@ def tile_modelnew_pa_kernel(tc, x, weight, bias, out):
 
         for part in range(FIRST_PARTS):
             load_weights(0, part, FIRST_PARTS)
+        bias_bf = keep.tile([P, O_TILES], BF16, name="bias_bf")
         for n in range(IMAGES):
             nc.sync.dma_start(out=x_raw[n], in_=x[n].rearrange("(q j) h w -> q j (h w)", j=PACK))
+            if n == PAIR - 1:
+                with nc.allow_non_contiguous_dma(reason="512 bias values, one to a partition and o-tile"):
+                    nc.sync.dma_start(out=bias_bf, in_=bias.rearrange("(k p) -> p k", p=P))
         for o_tile in range(1, O_TILES):
             load_weights(o_tile)
-
-        bias_bf = keep.tile([P, O_TILES], BF16, name="bias_bf")
-        with nc.allow_non_contiguous_dma(reason="512 bias values, one to a partition and o-tile"):
-            nc.scalar.dma_start(out=bias_bf, in_=bias.rearrange("(k p) -> p k", p=P))
 
         warm = keep.tile([P, 1], F32, name="warm")
         nc.scalar.activation(out=warm, in_=identity[:, 0:1], func=ACT.Sigmoid)
@@ -191,10 +193,14 @@ def tile_modelnew_pa_kernel(tc, x, weight, bias, out):
         x_codes = keep.tile([P, PAIRS, 4, COLS], U32, name="x_codes", align_bytes=64)
         x_scales = keep.tile([P, PAIRS, 4, COLS], U8, name="x_scales", align_bytes=64)
 
+        def gpsimd_copy(out, in_):
+            nc.gpsimd.tensor_scalar(out=out, in0=in_, scalar1=1.0, scalar2=0.0, op0=ALU.mult, op1=ALU.add)
+
         def regroup_x(copy, grouped, n, which):
-            by_parity = x_raw[n].rearrange("p j (a r b i s) -> p r s a b j i", r=2, b=OUT_SIDE // NEAR, i=NEAR, s=2)
+            near = 1 if copy is gpsimd_copy else NEAR
+            by_parity = x_raw[n].rearrange("p j (a r b i s) -> p r s a b j i", r=2, b=OUT_SIDE // near, i=near, s=2)
             copy(
-                out=grouped[:, n % PAIR].rearrange("p (a b i) j -> p a b j i", b=OUT_SIDE // NEAR, i=NEAR),
+                out=grouped[:, n % PAIR].rearrange("p (a b i) j -> p a b j i", b=OUT_SIDE // near, i=near),
                 in_=by_parity[:, which // 2, which % 2],
             )
 
@@ -217,24 +223,31 @@ def tile_modelnew_pa_kernel(tc, x, weight, bias, out):
                 sort_weights(weights[0], bunch, "V", part, FIRST_PARTS)
         bias_t = keep.tile([P, O_TILES], F32, name="bias_t")
         bias_t3 = keep.tile([P, O_TILES], F32, name="bias_t3")
-        nc.vector.tensor_scalar_add(out=bias_t, in0=bias_bf, scalar1=-0.5)
-        nc.vector.tensor_scalar_add(out=bias_t3, in0=bias_bf, scalar1=2.5)
 
         for bunch in FIRST_BUNCH_ORDER:
             transpose_weights(weights[0], bunch)
             copy_weights(weights[0], bunch)
         x_first, x_second = new_x_tiles(), new_x_tiles()
+        for which in X1_ON_SCALAR:
+            regroup_x(nc.scalar.copy, x_first[which], 1, which)
         for which in range(4):
             regroup_x(nc.vector.tensor_copy, x_first[which], 0, which)
         for bunch in FIRST_BUNCH_ORDER:
             quantise_weights(weights[0], bunch)
         regroup_x(nc.vector.tensor_copy, x_first[0], 1, 0)
         for which, then in ((1, 0), (3, 1), (2, 3)):
-            regroup_x(nc.vector.tensor_copy, x_first[which], 1, which)
+            if which not in X1_ON_SCALAR:
+                regroup_x(nc.vector.tensor_copy, x_first[which], 1, which)
             quantise_x(x_first[then], 0, then)
+            if then == 0:
+                nc.vector.tensor_scalar_add(out=bias_t, in0=bias_bf, scalar1=-0.5)
+                nc.vector.tensor_scalar_add(out=bias_t3, in0=bias_bf, scalar1=2.5)
         quantise_x(x_first[2], 0, 2)
 
-        for bunch in (2, 3, 0, 1):
+        sort_weights(weights[1], 2, "G")
+        for which in X3_ON_GPSIMD:
+            regroup_x(gpsimd_copy, x_second[which], IMAGES - 1, which)
+        for bunch in (0, 3):
             sort_weights(weights[1], bunch, "G")
 
         for which in X_CLASS_ORDER[:EARLY_X_CLASSES]:
@@ -414,6 +427,8 @@ def tile_modelnew_pa_kernel(tc, x, weight, bias, out):
             if i == 0:
                 for k, which in enumerate(X_CLASS_ORDER):
                     for n in range(PAIR + (1 if k < EARLY_X_CLASSES else 0), IMAGES):
+                        if n == IMAGES - 1 and which in X3_ON_GPSIMD:
+                            continue
                         if n == IMAGES - 1 and k >= IMAGES - VECTOR_LATE_CLASSES:
                             vector_jobs.append((regroup_x, nc.vector.tensor_copy, x_second[which], n, which))
                         else:

@@ -39,7 +39,7 @@ FLIP_POSITION = 0
 JOB_POSITION = 3
 X3_ON_GPSIMD = (2,)
 X1_ON_SCALAR = (3,)
-RELU_ON_SCALAR = (1, 2, 3)
+RELU_ON_SCALAR = (1, 2, 3, 4)
 BUNCH_ORDER = [2, 4, 0, 3, 1]
 BATCH_LAST = (5,)
 LOG_TURN, TANH_TURN = 2, 3
@@ -78,6 +78,10 @@ def as_images(flat):
 
 def image(flat, n):
     return flat[:, n * OUT_PIXELS : (n + 1) * OUT_PIXELS]
+
+
+def cut(split, *flats):
+    return [tuple(image(flat, n) for flat in flats) for n in range(PAIR)] if split else [flats]
 
 
 def tap_source(sums, kh, kw):
@@ -125,12 +129,13 @@ def tile_modelnew_pa_kernel(tc, x, weight, bias, out):
 
         for part in range(FIRST_PARTS):
             load_weights(0, part, FIRST_PARTS)
-        bias_bf = keep.tile([P, O_TILES], BF16, name="bias_bf")
+        bias_rows = keep.tile([P, P], BF16, name="bias_rows")
+        bias_wide = keep.tile([P, P], F32, name="bias_wide")
+        nc.gpsimd.memset(bias_rows, 0.0)
         for n in range(IMAGES):
             nc.sync.dma_start(out=x_raw[n], in_=x[n].rearrange("(q j) h w -> q j (h w)", j=PACK))
             if n == PAIR - 1:
-                with nc.allow_non_contiguous_dma(reason="512 bias values, one to a partition and o-tile"):
-                    nc.sync.dma_start(out=bias_bf, in_=bias.rearrange("(k p) -> p k", p=P))
+                nc.sync.dma_start(out=bias_rows[0:O_TILES], in_=bias.rearrange("(k p) -> k p", p=P))
         for o_tile in range(1, O_TILES):
             load_weights(o_tile)
 
@@ -234,14 +239,17 @@ def tile_modelnew_pa_kernel(tc, x, weight, bias, out):
             regroup_x(nc.vector.tensor_copy, x_first[which], 0, which)
         for bunch in FIRST_BUNCH_ORDER:
             quantise_weights(weights[0], bunch)
+        nc.vector.tensor_copy(out=bias_wide, in_=bias_rows)
+        turned = psum.tile([P, P], F32, name="sums")
+        nc.tensor.transpose(turned, bias_wide, identity)
         regroup_x(nc.vector.tensor_copy, x_first[0], 1, 0)
         for which, then in ((1, 0), (3, 1), (2, 3)):
             if which not in X1_ON_SCALAR:
                 regroup_x(nc.vector.tensor_copy, x_first[which], 1, which)
-            quantise_x(x_first[then], 0, then)
             if then == 0:
-                nc.vector.tensor_scalar_add(out=bias_t, in0=bias_bf, scalar1=-0.5)
-                nc.vector.tensor_scalar_add(out=bias_t3, in0=bias_bf, scalar1=2.5)
+                nc.vector.tensor_scalar_add(out=bias_t, in0=turned[:, 0:O_TILES], scalar1=-0.5)
+                nc.vector.tensor_scalar_add(out=bias_t3, in0=turned[:, 0:O_TILES], scalar1=2.5)
+            quantise_x(x_first[then], 0, then)
         quantise_x(x_first[2], 0, 2)
 
         sort_weights(weights[1], 2, "G")
@@ -300,50 +308,51 @@ def tile_modelnew_pa_kernel(tc, x, weight, bias, out):
             used = used_rows(folded, tap[0])
             nc.scalar.activation(out=used, in_=used, func=ACT.Abs, bias=-1.5, scale=1.0)
 
-        def fold_max(unit, folded, tap):
-            target, source = tap_target(unit["folded"], tap[0], tap[1]), tap_source(folded, tap[0], tap[1])
-            for n in range(PAIR):
-                nc.vector.tensor_tensor(out=target[:, n], in0=source[:, n], in1=target[:, n], op=ALU.max)
+        def max_into(target, source, split):
+            for n in range(PAIR if split else 1):
+                part = (slice(None), n) if split else slice(None)
+                nc.vector.tensor_tensor(out=target[part], in0=source[part], in1=target[part], op=ALU.max)
 
-        def fold_max_left(left, folded, tap):
-            target, source = target_rows(left, tap[0]), used_rows(folded, tap[0])
-            for n in range(PAIR):
-                nc.vector.tensor_tensor(out=target[:, n], in0=source[:, n], in1=target[:, n], op=ALU.max)
+        def fold_max(unit, folded, tap, split=True):
+            max_into(tap_target(unit["folded"], tap[0], tap[1]), tap_source(folded, tap[0], tap[1]), split)
+
+        def fold_max_left(left, folded, tap, split=True):
+            max_into(target_rows(left, tap[0]), used_rows(folded, tap[0]), split)
 
         def relu_smallest_scalar(unit):
             nc.scalar.activation(out=unit["smallest"], in_=unit["smallest"], func=ACT.Relu, bias=3.0, scale=1.0)
 
-        def relu_smallest(unit):
-            for n in range(PAIR):
-                smallest = image(unit["smallest"], n)
+        def relu_smallest(unit, split=True):
+            for smallest in cut(split, unit["smallest"]):
+                smallest = smallest[0]
                 nc.vector.tensor_scalar(out=smallest, in0=smallest, scalar1=3.0, scalar2=0.0, op0=ALU.add, op1=ALU.max)
 
-        def best_of_extremes(unit):
-            for n in range(PAIR):
-                smallest, largest = image(unit["smallest"], n), image(unit["largest"], n)
+        def best_of_extremes(unit, split=True):
+            for smallest, largest in cut(split, unit["smallest"], unit["largest"]):
                 nc.vector.scalar_tensor_tensor(
                     out=largest, in0=smallest, scalar=-1.0, in1=largest, op0=ALU.mult, op1=ALU.max
                 )
 
-        def merge_folded(unit):
-            for n in range(PAIR):
-                folded, largest = image(unit["folded"], n), image(unit["largest"], n)
+        def merge_folded(unit, split=True):
+            for folded, largest in cut(split, unit["folded"], unit["largest"]):
                 nc.vector.scalar_tensor_tensor(
                     out=largest, in0=folded, scalar=-1.5, in1=largest, op0=ALU.add, op1=ALU.max
                 )
 
-        def clip(unit):
-            for n in range(PAIR):
+        def clip(unit, split=True):
+            for smallest, largest in cut(split, unit["smallest"], unit["largest"]):
                 nc.vector.tensor_scalar(
-                    out=image(unit["smallest"], n), in0=image(unit["largest"], n),
+                    out=smallest, in0=largest,
                     scalar1=3.0, scalar2=6.0, op0=ALU.add, op1=ALU.min,
                 )
 
-        def hardswish_times_six(unit, engine):
-            engine.tensor_tensor(out=unit["six_m"], in0=unit["largest"], in1=unit["smallest"], op=ALU.mult)
+        def hardswish_times_six(unit, engine, split=False):
+            for six_m, largest, smallest in cut(split, unit["six_m"], unit["largest"], unit["smallest"]):
+                engine.tensor_tensor(out=six_m, in0=largest, in1=smallest, op=ALU.mult)
 
-        def sigmoid_gate(unit):
-            nc.scalar.activation(out=unit["gate"], in_=unit["six_m"], func=ACT.Sigmoid, scale=-1.0 / 6.0)
+        def sigmoid_gate(unit, split=False):
+            for gate, six_m in cut(split, unit["gate"], unit["six_m"]):
+                nc.scalar.activation(out=gate, in_=six_m, func=ACT.Sigmoid, scale=-1.0 / 6.0)
 
         def log_gate(unit):
             nc.scalar.activation(out=unit["gate"], in_=unit["gate"], func=ACT.Ln, bias=LOG_FLOOR, scale=1.0)
@@ -361,14 +370,19 @@ def tile_modelnew_pa_kernel(tc, x, weight, bias, out):
                 gate = image(unit["gate"], n)
                 nc.vector.scalar_tensor_tensor(out=gate, in0=gate, scalar=2.0, in1=gate, op0=ALU.add, op1=ALU.mult)
 
-        def root_gate(unit):
-            nc.scalar.activation(out=unit["gate"], in_=unit["gate"], func=ACT.Abs_reciprocal_sqrt, bias=9.0, scale=9.0)
+        def root_gate(unit, split):
+            for (gate,) in cut(split, unit["gate"]):
+                nc.scalar.activation(out=gate, in_=gate, func=ACT.Abs_reciprocal_sqrt, bias=9.0, scale=9.0)
 
-        def finish_root(unit):
-            nc.vector.scalar_tensor_tensor(
-                out=unit["gate"], in0=unit["gate"], scalar=-1.0 / 6.0, in1=unit["six_m"], op0=ALU.add, op1=ALU.mult
-            )
-            nc.sync.dma_start(out=unit["out"], in_=unit["gate"].rearrange("p (i x) -> p i x", i=PAIR))
+        def finish_root(unit, split):
+            for n, (gate, six_m) in enumerate(cut(split, unit["gate"], unit["six_m"])):
+                nc.vector.scalar_tensor_tensor(
+                    out=gate, in0=gate, scalar=-1.0 / 6.0, in1=six_m, op0=ALU.add, op1=ALU.mult
+                )
+                if split:
+                    nc.sync.dma_start(out=unit["out"][:, n], in_=gate)
+                else:
+                    nc.sync.dma_start(out=unit["out"], in_=gate.rearrange("p (i x) -> p i x", i=PAIR))
 
         def finish(unit):
             nc.vector.scalar_tensor_tensor(
@@ -397,6 +411,21 @@ def tile_modelnew_pa_kernel(tc, x, weight, bias, out):
 
         def call(step):
             step[0](*step[1:])
+
+        def touches(step):
+            if step[0] is fold_max_left:
+                return ("left",), "left"
+            if step[0] is fold_max:
+                return ("folded",) + (("left",) if step[3] == LEFT_SEED else ()), "folded"
+            if step[0] is relu_smallest:
+                return ("smallest",), "smallest"
+            if step[0] is best_of_extremes:
+                return ("smallest", "largest"), "largest"
+            if step[0] is merge_folded:
+                return ("folded", "largest"), "largest"
+            if step[0] is clip:
+                return ("largest",), "smallest"
+            return None
 
         for i in range(n_units + 2):
             now = None
@@ -441,7 +470,7 @@ def tile_modelnew_pa_kernel(tc, x, weight, bias, out):
             if i == n_units:
                 vector_jobs = [(square_gate, units[-2]), (widen_gate, units[-2])] + vector_jobs + [(square_gate, units[-1]), (widen_gate, units[-1])]
             if i == n_units + 1:
-                vector_jobs = [(finish_root, unit) for unit in units[-2:]]
+                vector_jobs = [(finish_root, units[-2], False), (finish_root, units[-1], True)]
 
             folds = FOLD_TAPS[: fold_count(i)] if now is not None else []
             extremes = [tap for tap in ALL_TAPS if tap != CENTRE and tap not in folds] if now is not None else []
@@ -476,14 +505,14 @@ def tile_modelnew_pa_kernel(tc, x, weight, bias, out):
             for unit in tanhs:
                 tanh_gate(unit)
             if i == n_units + 1:
-                for unit in units[-2:]:
-                    root_gate(unit)
+                root_gate(units[-2], False)
+                root_gate(units[-1], True)
             for step in scalar_jobs[:1]:
                 call(step)
             if now is not None and i in RELU_ON_SCALAR:
                 relu_smallest_scalar(now)
             if before is not None:
-                sigmoid_gate(before)
+                sigmoid_gate(before, i == n_units)
             for step in scalar_jobs[1:]:
                 call(step)
             for flip in late_flips:
@@ -508,19 +537,29 @@ def tile_modelnew_pa_kernel(tc, x, weight, bias, out):
                 else:
                     chain += [(merge_folded, now), (clip, now)]
                     between = [(relu_smallest, now), (best_of_extremes, now)]
+            early_low = []
             if 0 < len(chain) < 4 and between:
-                call(between[0])
+                early_low = between[:1]
                 between = between[1:]
             room = max(len(chain) - 1 - len(between), 0)
             first_jobs = max(len(vector_jobs) - room, 0)
-            for step in vector_jobs[:first_jobs]:
-                call(step)
             between += vector_jobs[first_jobs:]
+            steps = vector_jobs[:first_jobs]
             for k in range(len(chain)):
-                call(chain[k])
+                steps.append(chain[k])
                 if k < len(between):
-                    call(between[k])
+                    steps.append(between[k])
             if now is not None:
-                hardswish_times_six(now, nc.gpsimd if i < n_units - 1 else nc.vector)
+                steps = early_low + steps
+            touched = [touches(step) for step in steps]
+            for k, step in enumerate(steps):
+                if touched[k] is None:
+                    call(step)
+                    continue
+                behind = k > 0 and touched[k - 1] is not None and touched[k - 1][1] in touched[k][0]
+                ahead = k + 1 < len(steps) and touched[k + 1] is not None and touched[k][1] in touched[k + 1][0]
+                call(step + (bool(behind or ahead or (k == len(steps) - 1 and i == n_units - 1)),))
+            if now is not None:
+                hardswish_times_six(now, nc.gpsimd if i < n_units - 1 else nc.vector, i == n_units - 1)
             for step in gpsimd_jobs:
                 call(step)

@@ -43,7 +43,7 @@ RELU_ON_SCALAR = (1, 2, 3, 4)
 BUNCH_ORDER = [2, 4, 0, 3, 1]
 BATCH_LAST = (5,)
 LOG_TURN, TANH_TURN = 2, 3
-FOLDS_BY_TURN = (2, 4, 4, 4, 4, 5, 4, 4)
+FOLDS_BY_TURN = (2, 4, 4, 4, 4, 5, 3, 4)
 EARLY_X_CLASSES = 2
 VECTOR_LATE_CLASSES = 2
 NEAR = 4

from contextlib import ExitStack

import concourse.mybir as mybir
from concourse.masks import make_identity

F32 = mybir.dt.float32
BF16 = mybir.dt.bfloat16
U32 = mybir.dt.uint32
U8 = mybir.dt.uint8
FP8X4 = mybir.dt.float8_e4m3fn_x4
ALU = mybir.AluOpType
ACT = mybir.ActivationFunctionType

P = 128
PACK = 4
IMAGES, C_IN, SIDE = 4, 512, 32
C_OUT, KERNEL = 512, 3
TAPS = KERNEL * KERNEL
OUT_SIDE = SIDE // 2
OUT_PIXELS = OUT_SIDE * OUT_SIDE
PAIR = 2
PAIRS = IMAGES // PAIR
COLS = PAIR * OUT_PIXELS
O_TILES = C_OUT // P
HALVES = 2
BUNCH = 2
BUNCHES = (TAPS + BUNCH - 1) // BUNCH
LOG_FLOOR = 1e-18

CENTRE = (1, 1)
LEFT_SEED = (2, 0)
ALL_TAPS = [(1, 1), (1, 2), (2, 1), (0, 1), (0, 2), (1, 0), (2, 0), (0, 0), (2, 2)]
FOLD_TAPS = [(2, 2), (0, 0), (2, 0), (1, 0), (0, 2), (0, 1)]
FOLD_TILES = 6
SORTS_BY_LEAD = {4: [2], 3: [0, 3], 2: [1]}
FIRST_BUNCHES = 2
FLIP_BANKS = 2
FLIP_POSITION = 0
JOB_POSITION = 3
X3_ON_GPSIMD = (2,)
X1_ON_SCALAR = (3,)
RELU_ON_SCALAR = (1, 2, 3, 4)
BUNCH_ORDER = [2, 4, 0, 3, 1]
BATCH_LAST = (5,)
LOG_TURN, TANH_TURN = 2, 3
FOLDS_BY_TURN = (2, 4, 4, 4, 4, 5, 3, 4)
EARLY_X_CLASSES = 2
VECTOR_LATE_CLASSES = 2
NEAR = 4
FIRST_PARTS = 2
FIRST_BUNCH_ORDER = (2, 3, 4, 0, 1)
X_CLASS_ORDER = (0, 3, 1, 2)


def fold_count(i):
    return FOLDS_BY_TURN[i]


def batch_of(units, last):
    first = 0
    for other in BATCH_LAST:
        if other < last:
            first = other + 1
    return units[first : last + 1]


FLOPS = 2 * TAPS * IMAGES * OUT_PIXELS * C_OUT * C_IN


def tap_geometry(k):
    shift, parity = divmod(k - 1, 2)
    return shift, parity


def as_images(flat):
    return flat.rearrange("p (i a b) -> p i a b", i=PAIR, a=OUT_SIDE)


def image(flat, n):
    return flat[:, n * OUT_PIXELS : (n + 1) * OUT_PIXELS]


def cut(split, *flats):
    return [tuple(image(flat, n) for flat in flats) for n in range(PAIR)] if split else [flats]


def tap_source(sums, kh, kw):
    return as_images(sums)[:, :, 0 : OUT_SIDE + tap_geometry(kh)[0], 0 : OUT_SIDE + tap_geometry(kw)[0]]


def tap_target(running, kh, kw):
    return as_images(running)[:, :, -tap_geometry(kh)[0] : OUT_SIDE, -tap_geometry(kw)[0] : OUT_SIDE]


def used_rows(flat, kh):
    return as_images(flat)[:, :, 0 : OUT_SIDE + tap_geometry(kh)[0], :]


def target_rows(flat, kh):
    return as_images(flat)[:, :, -tap_geometry(kh)[0] : OUT_SIDE, :]


def tile_modelnew_pa_kernel(tc, x, weight, bias, out):
    nc = tc.nc
    with ExitStack() as stack:
        keep = stack.enter_context(tc.tile_pool(name="keep", bufs=1))
        x_stage = stack.enter_context(tc.tile_pool(name="x_stage", bufs=5))
        w_stage = stack.enter_context(tc.tile_pool(name="w_stage", bufs=2))
        w_ready = stack.enter_context(tc.tile_pool(name="w_ready", bufs=2))
        stats = stack.enter_context(tc.tile_pool(name="stats", bufs=3))
        late = stack.enter_context(tc.tile_pool(name="late", bufs=8))
        psum = stack.enter_context(tc.psum_pool(name="psum", bufs=6))
        psum_w = stack.enter_context(tc.psum_pool(name="psum_w", bufs=2))
        stack.enter_context(tc.manual_schedule())

        identity = keep.tile([P, P], F32, name="identity")
        make_identity(nc, identity)

        w_rows = [keep.tile([P, C_IN * TAPS], BF16, name="w_rows%d" % o_tile) for o_tile in range(O_TILES)]
        x_raw = [keep.tile([P, PACK, SIDE * SIDE], BF16, name="x_raw%d" % n) for n in range(IMAGES)]

        def load_weights(o_tile, part=0, parts=1):
            width = C_IN * TAPS // parts
            cols = slice(part * width, (part + 1) * width)
            nc.sync.dma_start(
                out=w_rows[o_tile][:, cols],
                in_=weight[o_tile * P : (o_tile + 1) * P].rearrange("o c kh kw -> o (c kh kw)")[:, cols],
            )

        for part in range(FIRST_PARTS):
            load_weights(0, part, FIRST_PARTS)
        bias_rows = keep.tile([P, P], BF16, name="bias_rows")
        bias_wide = keep.tile([P, P], F32, name="bias_wide")
        nc.gpsimd.memset(bias_rows, 0.0)
        for n in range(IMAGES):
            nc.sync.dma_start(out=x_raw[n], in_=x[n].rearrange("(q j) h w -> q j (h w)", j=PACK))
            if n == PAIR - 1:
                nc.sync.dma_start(out=bias_rows[0:O_TILES], in_=bias.rearrange("(k p) -> k p", p=P))
        for o_tile in range(1, O_TILES):
            load_weights(o_tile)

        warm = keep.tile([P, 1], F32, name="warm")
        nc.scalar.activation(out=warm, in_=identity[:, 0:1], func=ACT.Sigmoid)

        def new_weights(o_tile):
            return {"rows": w_rows[o_tile].rearrange("o (c t) -> o c t", t=TAPS)}

        def sort_weights(w, bunch, engine="V", part=0, parts=1):
            if "sorted" not in w:
                by_tap = w_stage.tile([P, TAPS, C_IN], BF16, name="w_sorted")
                w["sorted"] = by_tap
                w["words"] = by_tap.rearrange("o t c -> o (t c)").bitcast(F32).rearrange("o (t q u) -> o t q u", t=TAPS, u=HALVES)
            t0, t1 = bunch * BUNCH, min((bunch + 1) * BUNCH, TAPS)
            c = slice(part * C_IN // parts, (part + 1) * C_IN // parts)
            out_view = w["sorted"][:, t0:t1, c].rearrange("o t c -> o c t")
            in_view = w["rows"][:, c, t0:t1]
            if engine == "S":
                nc.scalar.copy(out=out_view, in_=in_view)
            elif engine == "G":
                nc.gpsimd.tensor_scalar(
                    out=out_view, in0=in_view, scalar1=1.0, scalar2=0.0, op0=ALU.mult, op1=ALU.add
                )
            else:
                nc.vector.tensor_copy(out=out_view, in_=in_view)

        def transpose_weights(w, bunch):
            t0, t1 = bunch * BUNCH, min((bunch + 1) * BUNCH, TAPS)
            flipped = psum_w.tile([P, BUNCH, HALVES, P], F32, name="flipped")
            w["flipped%d" % bunch] = flipped
            for t in range(t0, t1):
                for u in range(HALVES):
                    nc.tensor.transpose(
                        flipped[:, t - t0, u, :], w["words"][:, t, :, u], identity
                    )

        def copy_weights(w, bunch):
            if "grouped" not in w:
                w["grouped"] = w_stage.tile([P, TAPS, P * PACK], BF16, name="w_grouped", align_bytes=64)
            t0, t1 = bunch * BUNCH, min((bunch + 1) * BUNCH, TAPS)
            flipped = w["flipped%d" % bunch]
            words = w["grouped"][:, t0:t1, :].rearrange("q t k -> q (t k)").bitcast(F32)
            nc.scalar.copy(
                out=words.rearrange("q (t o u) -> q t o u", t=t1 - t0, u=HALVES),
                in_=flipped[:, 0 : t1 - t0].rearrange("q t u o -> q t o u"),
            )

        def quantise_weights(w, bunch):
            if "codes" not in w:
                w["codes"] = w_ready.tile([P, TAPS, P], U32, name="w_codes", align_bytes=64)
                w["scales"] = w_ready.tile([P, TAPS, P], U8, name="w_scales", align_bytes=64)
            t0, t1 = bunch * BUNCH, min((bunch + 1) * BUNCH, TAPS)
            nc.vector.quantize_mx(
                out=w["codes"][:, t0:t1, :].rearrange("q t o -> q (t o)").bitcast(FP8X4),
                scales=w["scales"][:, t0:t1, :].rearrange("q t o -> q (t o)"),
                in_=w["grouped"][:, t0:t1, :].rearrange("q t k -> q (t k)"),
            )

        x_codes = keep.tile([P, PAIRS, 4, COLS], U32, name="x_codes", align_bytes=64)
        x_scales = keep.tile([P, PAIRS, 4, COLS], U8, name="x_scales", align_bytes=64)

        def gpsimd_copy(out, in_):
            nc.gpsimd.tensor_scalar(out=out, in0=in_, scalar1=1.0, scalar2=0.0, op0=ALU.mult, op1=ALU.add)

        def regroup_x(copy, grouped, n, which):
            near = 1 if copy is gpsimd_copy else NEAR
            by_parity = x_raw[n].rearrange("p j (a r b i s) -> p r s a b j i", r=2, b=OUT_SIDE // near, i=near, s=2)
            copy(
                out=grouped[:, n % PAIR].rearrange("p (a b i) j -> p a b j i", b=OUT_SIDE // near, i=near),
                in_=by_parity[:, which // 2, which % 2],
            )

        def quantise_x(grouped, pair, which):
            nc.vector.quantize_mx(
                out=x_codes[:, pair, which, :].bitcast(FP8X4),
                scales=x_scales[:, pair, which, :],
                in_=grouped.rearrange("p i x j -> p (i x j)"),
            )

        def new_x_tiles():
            return [
                x_stage.tile([P, PAIR, OUT_PIXELS, PACK], BF16, name="x_grouped%d" % which, bufs=2, align_bytes=64)
                for which in range(4)
            ]

        weights = [new_weights(o_tile) for o_tile in range(O_TILES)]
        for part in range(FIRST_PARTS):
            for bunch in FIRST_BUNCH_ORDER:
                sort_weights(weights[0], bunch, "V", part, FIRST_PARTS)
        bias_t = keep.tile([P, O_TILES], F32, name="bias_t")
        bias_t3 = keep.tile([P, O_TILES], F32, name="bias_t3")

        for bunch in FIRST_BUNCH_ORDER:
            transpose_weights(weights[0], bunch)
            copy_weights(weights[0], bunch)
        x_first, x_second = new_x_tiles(), new_x_tiles()
        for which in X1_ON_SCALAR:
            regroup_x(nc.scalar.copy, x_first[which], 1, which)
        for which in range(4):
            regroup_x(nc.vector.tensor_copy, x_first[which], 0, which)
        for bunch in FIRST_BUNCH_ORDER:
            quantise_weights(weights[0], bunch)
        nc.vector.tensor_copy(out=bias_wide, in_=bias_rows)
        turned = psum.tile([P, P], F32, name="sums")
        nc.tensor.transpose(turned, bias_wide, identity)
        regroup_x(nc.vector.tensor_copy, x_first[0], 1, 0)
        for which, then in ((1, 0), (3, 1), (2, 3)):
            if which not in X1_ON_SCALAR:
                regroup_x(nc.vector.tensor_copy, x_first[which], 1, which)
            if then == 0:
                nc.vector.tensor_scalar_add(out=bias_t, in0=turned[:, 0:O_TILES], scalar1=-0.5)
                nc.vector.tensor_scalar_add(out=bias_t3, in0=turned[:, 0:O_TILES], scalar1=2.5)
            quantise_x(x_first[then], 0, then)
        quantise_x(x_first[2], 0, 2)

        sort_weights(weights[1], 2, "G")
        for which in X3_ON_GPSIMD:
            regroup_x(gpsimd_copy, x_second[which], IMAGES - 1, which)
        for bunch in (0, 3):
            sort_weights(weights[1], bunch, "G")

        for which in X_CLASS_ORDER[:EARLY_X_CLASSES]:
            regroup_x(nc.scalar.copy, x_second[which], PAIR, which)

        def tap_sums(unit, tap):
            kh, kw = tap
            which = 2 * tap_geometry(kh)[1] + tap_geometry(kw)[1]
            t = kh * KERNEL + kw
            sums = psum.tile([P, COLS], F32, name="sums")
            nc.tensor.matmul_mx(
                out=sums,
                lhsT=unit["weights"]["codes"][:, t, :].bitcast(FP8X4),
                lhsT_scale=unit["weights"]["scales"][:, t, :],
                rhs=x_codes[:, unit["pair"], which, :].bitcast(FP8X4),
                rhs_scale=x_scales[:, unit["pair"], which, :],
                start=True,
                stop=True,
            )
            return sums

        def seed_extremes(unit):
            nc.scalar.activation(
                out=unit["seed"], in_=tap_sums(unit, CENTRE), func=ACT.Identity, bias=unit["bias_t"], scale=1.0
            )

        def extremes_tap(unit, tap, first):
            kh, kw = tap
            source = tap_source(tap_sums(unit, tap), kh, kw)
            low, high = (unit["seed"], unit["seed"]) if first else (unit["smallest"], unit["largest"])
            nc.vector.scalar_tensor_tensor(
                out=tap_target(unit["smallest"], kh, kw), in0=source, scalar=unit["bias_t"],
                in1=tap_target(low, kh, kw), op0=ALU.add, op1=ALU.min,
            )
            nc.vector.scalar_tensor_tensor(
                out=tap_target(unit["largest"], kh, kw), in0=source, scalar=unit["bias_t"],
                in1=tap_target(high, kh, kw), op0=ALU.add, op1=ALU.max,
            )

        def fold_relu(unit, tap, first):
            kh, kw = tap
            folded = unit["folded"] if first else stats.tile([P, COLS], F32, name="fold", bufs=FOLD_TILES)
            nc.scalar.activation(
                out=used_rows(folded, kh), in_=used_rows(tap_sums(unit, tap), kh),
                func=ACT.Relu, bias=unit["bias_t3"], scale=1.0,
            )
            return folded

        def fold_abs(folded, tap):
            used = used_rows(folded, tap[0])
            nc.scalar.activation(out=used, in_=used, func=ACT.Abs, bias=-1.5, scale=1.0)

        def max_into(target, source, split):
            for n in range(PAIR if split else 1):
                part = (slice(None), n) if split else slice(None)
                nc.vector.tensor_tensor(out=target[part], in0=source[part], in1=target[part], op=ALU.max)

        def fold_max(unit, folded, tap, split=True):
            max_into(tap_target(unit["folded"], tap[0], tap[1]), tap_source(folded, tap[0], tap[1]), split)

        def fold_max_left(left, folded, tap, split=True):
            max_into(target_rows(left, tap[0]), used_rows(folded, tap[0]), split)

        def relu_smallest_scalar(unit):
            nc.scalar.activation(out=unit["smallest"], in_=unit["smallest"], func=ACT.Relu, bias=3.0, scale=1.0)

        def relu_smallest(unit, split=True):
            for smallest in cut(split, unit["smallest"]):
                smallest = smallest[0]
                nc.vector.tensor_scalar(out=smallest, in0=smallest, scalar1=3.0, scalar2=0.0, op0=ALU.add, op1=ALU.max)

        def best_of_extremes(unit, split=True):
            for smallest, largest in cut(split, unit["smallest"], unit["largest"]):
                nc.vector.scalar_tensor_tensor(
                    out=largest, in0=smallest, scalar=-1.0, in1=largest, op0=ALU.mult, op1=ALU.max
                )

        def merge_folded(unit, split=True):
            for folded, largest in cut(split, unit["folded"], unit["largest"]):
                nc.vector.scalar_tensor_tensor(
                    out=largest, in0=folded, scalar=-1.5, in1=largest, op0=ALU.add, op1=ALU.max
                )

        def clip(unit, split=True):
            for smallest, largest in cut(split, unit["smallest"], unit["largest"]):
                nc.vector.tensor_scalar(
                    out=smallest, in0=largest,
                    scalar1=3.0, scalar2=6.0, op0=ALU.add, op1=ALU.min,
                )

        def hardswish_times_six(unit, engine, split=False):
            for six_m, largest, smallest in cut(split, unit["six_m"], unit["largest"], unit["smallest"]):
                engine.tensor_tensor(out=six_m, in0=largest, in1=smallest, op=ALU.mult)

        def sigmoid_gate(unit, split=False):
            for gate, six_m in cut(split, unit["gate"], unit["six_m"]):
                nc.scalar.activation(out=gate, in_=six_m, func=ACT.Sigmoid, scale=-1.0 / 6.0)

        def log_gate(unit):
            nc.scalar.activation(out=unit["gate"], in_=unit["gate"], func=ACT.Ln, bias=LOG_FLOOR, scale=1.0)

        def tanh_gate(unit):
            nc.scalar.activation(out=unit["gate"], in_=unit["gate"], func=ACT.Tanh, scale=-1.0)

        def square_gate(unit):
            for n in range(PAIR):
                gate = image(unit["gate"], n)
                nc.vector.tensor_tensor(out=gate, in0=gate, in1=gate, op=ALU.mult)

        def widen_gate(unit):
            for n in range(PAIR):
                gate = image(unit["gate"], n)
                nc.vector.scalar_tensor_tensor(out=gate, in0=gate, scalar=2.0, in1=gate, op0=ALU.add, op1=ALU.mult)

        def root_gate(unit, split):
            for (gate,) in cut(split, unit["gate"]):
                nc.scalar.activation(out=gate, in_=gate, func=ACT.Abs_reciprocal_sqrt, bias=9.0, scale=9.0)

        def finish_root(unit, split):
            for n, (gate, six_m) in enumerate(cut(split, unit["gate"], unit["six_m"])):
                nc.vector.scalar_tensor_tensor(
                    out=gate, in0=gate, scalar=-1.0 / 6.0, in1=six_m, op0=ALU.add, op1=ALU.mult
                )
                if split:
                    nc.sync.dma_start(out=unit["out"][:, n], in_=gate)
                else:
                    nc.sync.dma_start(out=unit["out"], in_=gate.rearrange("p (i x) -> p i x", i=PAIR))

        def finish(unit):
            nc.vector.scalar_tensor_tensor(
                out=unit["gate"], in0=unit["six_m"], scalar=1.0 / 6.0, in1=unit["gate"], op0=ALU.mult, op1=ALU.mult
            )
            nc.sync.dma_start(out=unit["out"], in_=unit["gate"].rearrange("p (i x) -> p i x", i=PAIR))

        n_units = O_TILES * PAIRS
        units = []

        def new_unit(i):
            o_tile, pair = divmod(i, PAIRS)
            return {
                "pair": pair,
                "out": out[pair * PAIR : (pair + 1) * PAIR, o_tile * P : (o_tile + 1) * P].rearrange("i o a b -> o i (a b)"),
                "weights": weights[o_tile],
                "bias_t": bias_t[:, o_tile : o_tile + 1],
                "bias_t3": bias_t3[:, o_tile : o_tile + 1],
                "seed": stats.tile([P, COLS], F32, name="seed"),
                "largest": stats.tile([P, COLS], F32, name="largest"),
                "smallest": stats.tile([P, COLS], F32, name="smallest"),
                "folded": stats.tile([P, COLS], F32, name="folded"),
                "six_m": late.tile([P, COLS], F32, name="six_m"),
                "gate": late.tile([P, COLS], F32, name="gate"),
            }

        def call(step):
            step[0](*step[1:])

        def touches(step):
            if step[0] is fold_max_left:
                return ("left",), "left"
            if step[0] is fold_max:
                return ("folded",) + (("left",) if step[3] == LEFT_SEED else ()), "folded"
            if step[0] is relu_smallest:
                return ("smallest",), "smallest"
            if step[0] is best_of_extremes:
                return ("smallest", "largest"), "largest"
            if step[0] is merge_folded:
                return ("folded", "largest"), "largest"
            if step[0] is clip:
                return ("largest",), "smallest"
            return None

        for i in range(n_units + 2):
            now = None
            if i < n_units:
                now = new_unit(i)
                units.append(now)
            before = units[i - 1] if 1 <= i <= n_units else None

            scalar_jobs, vector_jobs, gpsimd_jobs, late_flips, flips = [], [], [], [], []
            for o_tile in range(1, O_TILES):
                lead = o_tile * PAIRS - i
                gpsimd_jobs += [(sort_weights, weights[o_tile], bunch, "G") for bunch in SORTS_BY_LEAD.get(lead, [])]
                if lead == (2 if o_tile == 1 else 3):
                    scalar_jobs.append((sort_weights, weights[o_tile], 4, "S"))
                bunches = []
                if lead == 2:
                    bunches = BUNCH_ORDER[:FIRST_BUNCHES]
                if lead == 1:
                    bunches = BUNCH_ORDER[FIRST_BUNCHES:]
                if o_tile == 1 and lead == 2:
                    late_flips += [(weights[o_tile], bunch) for bunch in bunches]
                    continue
                if o_tile == 1 and lead == 1:
                    vector_jobs += [(quantise_weights, weights[o_tile], bunch) for bunch in BUNCH_ORDER[:FIRST_BUNCHES]]
                flips += [(weights[o_tile], bunch) for bunch in bunches]
                scalar_jobs += [(copy_weights, weights[o_tile], bunch) for bunch in bunches]
                vector_jobs += [(quantise_weights, weights[o_tile], bunch) for bunch in bunches]
            if i == 0:
                for k, which in enumerate(X_CLASS_ORDER):
                    for n in range(PAIR + (1 if k < EARLY_X_CLASSES else 0), IMAGES):
                        if n == IMAGES - 1 and which in X3_ON_GPSIMD:
                            continue
                        if n == IMAGES - 1 and k >= IMAGES - VECTOR_LATE_CLASSES:
                            vector_jobs.append((regroup_x, nc.vector.tensor_copy, x_second[which], n, which))
                        else:
                            scalar_jobs.append((regroup_x, nc.scalar.copy, x_second[which], n, which))
                vector_jobs += [(quantise_x, x_second[which], 1, which) for which in X_CLASS_ORDER]
            logs = [unit for last in BATCH_LAST if i == last + LOG_TURN for unit in batch_of(units, last)]
            tanhs = [unit for last in BATCH_LAST if i == min(last + TANH_TURN, n_units + 1) for unit in batch_of(units, last)]
            scalar_fill = [(log_gate, unit) for unit in logs]
            vector_jobs += [(finish, unit) for unit in tanhs]
            if i == n_units:
                vector_jobs = [(square_gate, units[-2]), (widen_gate, units[-2])] + vector_jobs + [(square_gate, units[-1]), (widen_gate, units[-1])]
            if i == n_units + 1:
                vector_jobs = [(finish_root, units[-2], False), (finish_root, units[-1], True)]

            folds = FOLD_TAPS[: fold_count(i)] if now is not None else []
            extremes = [tap for tap in ALL_TAPS if tap != CENTRE and tap not in folds] if now is not None else []

            if now is not None:
                seed_extremes(now)
            fold_tiles = []
            for position in range(max(len(folds), len(extremes))):
                if i == 0 and position < len(extremes):
                    extremes_tap(now, extremes[position], position == 0)
                if position < len(folds):
                    fold_tiles.append(fold_relu(now, folds[position], position == 0))
                    if position >= 1:
                        fold_abs(fold_tiles[position - 1], folds[position - 1])
                if i > 0 and position < len(extremes):
                    extremes_tap(now, extremes[position], position == 0)
                if position == FLIP_POSITION:
                    for flip in flips[:FLIP_BANKS]:
                        transpose_weights(*flip)
                if scalar_fill:
                    call(scalar_fill[0])
                    scalar_fill = scalar_fill[1:]
                elif scalar_jobs and position >= JOB_POSITION and (position - JOB_POSITION) % 2 == 0:
                    call(scalar_jobs[0])
                    scalar_jobs = scalar_jobs[1:]
            for flip in flips[FLIP_BANKS:]:
                transpose_weights(*flip)
            if folds:
                fold_abs(fold_tiles[-1], folds[-1])
            for step in scalar_fill:
                call(step)
            for unit in tanhs:
                tanh_gate(unit)
            if i == n_units + 1:
                root_gate(units[-2], False)
                root_gate(units[-1], True)
            for step in scalar_jobs[:1]:
                call(step)
            if now is not None and i in RELU_ON_SCALAR:
                relu_smallest_scalar(now)
            if before is not None:
                sigmoid_gate(before, i == n_units)
            for step in scalar_jobs[1:]:
                call(step)
            for flip in late_flips:
                transpose_weights(*flip)
                copy_weights(*flip)

            chain, between = [], []
            if now is not None:
                if LEFT_SEED in folds:
                    left = fold_tiles[folds.index(LEFT_SEED)]
                    chain = [
                        (fold_max_left, left, fold_tiles[k], folds[k])
                        for k in range(1, len(folds)) if folds[k][1] == 0 and folds[k] != LEFT_SEED
                    ]
                    chain += [(fold_max, now, fold_tiles[k], folds[k]) for k in range(1, len(folds)) if folds[k][1] != 0]
                    chain += [(fold_max, now, left, LEFT_SEED)]
                else:
                    chain = [(fold_max, now, fold_tiles[k], folds[k]) for k in range(1, len(folds))]
                if i in RELU_ON_SCALAR:
                    chain += [(merge_folded, now), (best_of_extremes, now), (clip, now)]
                    between = []
                else:
                    chain += [(merge_folded, now), (clip, now)]
                    between = [(relu_smallest, now), (best_of_extremes, now)]
            early_low = []
            if 0 < len(chain) < 4 and between:
                early_low = between[:1]
                between = between[1:]
            room = max(len(chain) - 1 - len(between), 0)
            first_jobs = max(len(vector_jobs) - room, 0)
            between += vector_jobs[first_jobs:]
            steps = vector_jobs[:first_jobs]
            for k in range(len(chain)):
                steps.append(chain[k])
                if k < len(between):
                    steps.append(between[k])
            if now is not None:
                steps = early_low + steps
            touched = [touches(step) for step in steps]
            for k, step in enumerate(steps):
                if touched[k] is None:
                    call(step)
                    continue
                behind = k > 0 and touched[k - 1] is not None and touched[k - 1][1] in touched[k][0]
                ahead = k + 1 < len(steps) and touched[k + 1] is not None and touched[k][1] in touched[k + 1][0]
                call(step + (bool(behind or ahead or (k == len(steps) - 1 and i == n_units - 1)),))
            if now is not None:
                hardswish_times_six(now, nc.gpsimd if i < n_units - 1 else nc.vector, i == n_units - 1)
            for step in gpsimd_jobs:
                call(step)
